import numpy as np
import ml_dtypes


def mxq(x, axis, fmt="e4m3"):
    dtype, down = {"e4m3": (ml_dtypes.float8_e4m3fn, 7), "e5m2": (ml_dtypes.float8_e5m2, 14)}[fmt]
    v = np.moveaxis(np.asarray(x, np.float32).astype(ml_dtypes.bfloat16).astype(np.float64), axis, -1)
    blocks = v.reshape(v.shape[:-1] + (-1, 32))
    amax = np.abs(blocks).max(-1, keepdims=True)
    byte = np.maximum(np.where(amax > 0, np.frexp(amax)[1] - 1 + 127, 0) - down, 1)
    scale = np.exp2(byte - 127.0)
    codes = (blocks / scale).astype(np.float32).astype(dtype).astype(np.float64)
    return np.moveaxis((codes * scale).reshape(v.shape), -1, axis)


WIDE = False


def mx_kscale(k):
    if not WIDE:
        return np.ones(k)
    levels = np.array([10, -10, 5, -5, 0])
    a = np.random.permutation(np.resize(levels, k // 512 * 4)).reshape(k // 512, 4)
    idx = np.arange(k)
    return np.exp2(a[idx // 512, idx % 128 // 32])


BF16 = ml_dtypes.bfloat16


def bf(x):
    return np.asarray(x, np.float32).astype(BF16)


def f64(x):
    return np.asarray(x).astype(np.float64)


E2M1 = np.array([0.0, 0.5, 1.0, 1.5, 2.0, 3.0, 4.0, 6.0, -0.0, -0.5, -1.0, -1.5, -2.0, -3.0, -4.0, -6.0])


def pack_weight(w, fmt):
    k, n = w.shape
    w = f64(bf(w)).reshape(k // 32, 32, n)
    amax = np.abs(w).max(1)
    if fmt == "e4m3":
        byte = np.frexp(amax)[1] - 1 + 127 - 7
    else:
        mant, ex = np.frexp(amax / 6.0)
        byte = np.where(mant > 0.5, ex, ex - 1) + 127
    byte = np.clip(np.where(amax > 0, byte, 1), 1, 254)
    scaled = (w * np.exp2(127.0 - byte)[:, None, :]).reshape(k, n).astype(np.float32)
    by_word = np.ascontiguousarray(scaled.reshape(k // 512, 128, 4, n).transpose(0, 1, 3, 2))
    if fmt == "e4m3":
        words = by_word.astype(ml_dtypes.float8_e4m3fn).view(np.uint8)
    else:
        c = by_word.astype(ml_dtypes.float4_e2m1fn).view(np.uint8) & 0xF
        words = c[..., 0::2] | (c[..., 1::2] << 4)
    return np.ascontiguousarray(words), np.ascontiguousarray(byte.astype(np.uint8).reshape(k // 512, 16, n))


def unpack_weight(words, scales, fmt):
    g, p, n, _ = words.shape
    if fmt == "e4m3":
        vals = np.ascontiguousarray(words).view(ml_dtypes.float8_e4m3fn).astype(np.float64)
    else:
        nib = np.empty((g, p, n, 4), np.uint8)
        nib[..., 0::2] = words & 0xF
        nib[..., 1::2] = words >> 4
        vals = E2M1[nib]
    vals = vals * np.repeat(np.exp2(scales.astype(np.float64) - 127.0), 8, axis=1)[..., None]
    return vals.transpose(0, 1, 3, 2).reshape(g * 512, n)


B, C, IN, H, ND, NG, NL = 4, 128, 1024, 512, 2, 4, 2
N = B * C
K = ND * H
USED = [0, 2, 3]


def sigmoid(v):
    return 1.0 / (1.0 + np.exp(-v))


def cell(inq, wt, b1, b2):
    wu = wt.reshape(-1, NG, H)[:, USED].reshape(-1, len(USED) * H)
    gates = (inq @ wu) + b1.reshape(NG, H)[USED].reshape(-1) + b2.reshape(NG, H)[USED].reshape(-1)
    i, g, o = np.split(gates, len(USED), axis=-1)
    c = sigmoid(i) * np.tanh(g)
    return sigmoid(o) * np.tanh(c)


def setup_inputs():
    s = mx_kscale(K)
    z = np.random.standard_normal((len(USED), N, K)) * 1.5
    h = sigmoid(z[2]) * np.tanh(sigmoid(z[0]) * np.tanh(z[1]))
    w = np.random.standard_normal((NL, ND, NG * H, K)) * 7.0 / np.sqrt(K)
    w[0] = w[0] / s
    cat = np.swapaxes(w, -1, -2).reshape(-1, NG * H)
    words, scales = pack_weight(cat, "e4m3")
    return {"h_layer0": bf(h * s), "w_ih_words": words, "w_ih_scales": scales,
            "b_ih": bf(np.random.standard_normal((NL, ND, NG * H)) * 0.3),
            "b_hh": bf(np.random.standard_normal((NL, ND, NG * H)) * 0.3)}


def reference(h_layer0, w_ih_words, w_ih_scales, b_ih, b_hh):
    h = f64(h_layer0)
    wt = unpack_weight(w_ih_words, w_ih_scales, "e4m3").reshape(NL, ND, K, NG * H)
    b1, b2 = f64(b_ih), f64(b_hh)
    for l in range(NL):
        hq = mxq(h, 1, "e4m3")
        h = np.concatenate([cell(hq, wt[l, d], b1[l, d], b2[l, d]) for d in range(ND)], axis=-1)
    return h.reshape(B, C, ND * H)

@@ -1,0 +1,275 @@
+from contextlib import ExitStack
+
+import concourse.mybir as mybir
+from concourse.masks import make_identity
+
+F32 = mybir.dt.float32
+BF16 = mybir.dt.bfloat16
+I32 = mybir.dt.int32
+U32 = mybir.dt.uint32
+U8 = mybir.dt.uint8
+FP8X4 = mybir.dt.float8_e4m3fn_x4
+SIGMOID = mybir.ActivationFunctionType.Sigmoid
+TANH = mybir.ActivationFunctionType.Tanh
+MULT = mybir.AluOpType.mult
+ADD = mybir.AluOpType.add
+
+P = 128
+PACK = 4
+K_PASS = P * PACK
+TOKENS = 512
+FEATURES = 1024
+HIDDEN = 512
+LAYERS = 2
+DIRECTIONS = 2
+PASSES = FEATURES // K_PASS
+GATE_BLOCKS = 4
+BLOCK_I, BLOCK_G, BLOCK_O = 0, 2, 3
+TILES_PER_BLOCK = HIDDEN // P
+CHUNK = 256
+CHUNKS = TOKENS // CHUNK
+TOKEN_TILES = CHUNK // P
+PAIR = 2
+PAIRS = TILES_PER_BLOCK // PAIR
+UNITS_PER_CHUNK = DIRECTIONS * PAIRS
+UNITS_PER_LAYER = CHUNKS * UNITS_PER_CHUNK
+UNITS = LAYERS * UNITS_PER_LAYER
+AHEAD = 2
+HALVES = LAYERS * CHUNKS * PASSES
+FIRST_STEP = -2 * AHEAD
+
+FLOPS = 2 * TOKENS * FEATURES * 3 * HIDDEN * LAYERS * DIRECTIONS
+BYTES = (
+    TOKENS * FEATURES * 2
+    + LAYERS * DIRECTIONS * FEATURES * 3 * HIDDEN
+    + LAYERS * DIRECTIONS * (FEATURES // 32) * 3 * HIDDEN
+    + 2 * LAYERS * DIRECTIONS * 3 * HIDDEN * 2
+    + TOKENS * FEATURES * 4
+)
+
+
+def unit_place(unit):
+    layer, rest = divmod(unit, UNITS_PER_LAYER)
+    chunk, rest = divmod(rest, UNITS_PER_CHUNK)
+    direction, pair = divmod(rest, PAIRS)
+    return layer, chunk, direction, pair
+
+
+def half_place(half):
+    layer, rest = divmod(half, CHUNKS * PASSES)
+    chunk, k_pass = divmod(rest, PASSES)
+    return layer, chunk, k_pass
+
+
+def tile_lstmnetwork_pb_e_kernel(tc, h_layer0, w_ih_words, w_ih_scales, b_ih, b_hh, out):
+    nc = tc.nc
+    out_rows = out.rearrange("b c f -> (b c) f")
+    parked = [
+        out_rows[c * CHUNK : (c + 1) * CHUNK, :].rearrange("r (a n) -> (r a) n", n=CHUNK) for c in range(CHUNKS)
+    ]
+
+    with ExitStack() as ctx:
+        ctx.enter_context(tc.manual_schedule())
+        keep = ctx.enter_context(tc.tile_pool(name="keep", bufs=1))
+        stage = ctx.enter_context(tc.tile_pool(name="stage", bufs=2))
+        work = ctx.enter_context(tc.tile_pool(name="work", bufs=2))
+        leave = ctx.enter_context(tc.tile_pool(name="leave", bufs=3))
+        gate_banks = ctx.enter_context(tc.psum_pool(name="gate_banks", bufs=AHEAD))
+        turn_banks = ctx.enter_context(tc.psum_pool(name="turn_banks", bufs=2))
+
+        x_rows = [keep.tile([P, TOKEN_TILES, FEATURES], BF16, name="x_rows%d" % c) for c in range(CHUNKS)]
+        w_words = [
+            keep.tile([P, GATE_BLOCKS * HIDDEN * PACK], U8, name="w_words%d" % e, align_bytes=64)
+            for e in range(LAYERS * DIRECTIONS * PASSES)
+        ]
+        w_planes = [keep.tile([P, GATE_BLOCKS * HIDDEN], U8, name="w_planes%d" % l, align_bytes=64) for l in range(LAYERS)]
+        h_words = keep.tile([P, HALVES, CHUNK], U32, align_bytes=64)
+        h_planes = keep.tile([P, HALVES, CHUNK], U8, align_bytes=64)
+        identity = keep.tile([P, P], F32)
+        bias_rows = keep.tile([P, P], BF16)
+        bias_rows_f32 = keep.tile([P, P], F32)
+        bias_ih = keep.tile([P, P // 2], F32)
+        bias = keep.tile([P, P // 2], F32)
+        warm_in = keep.tile([P, 1], F32)
+        warm_out = keep.tile([P, 1], F32)
+
+        nc.scalar.dma_start(out=bias_rows[0 : P // 2, :], in_=b_ih.rearrange("l d (r c) -> (l d r) c", c=P))
+        nc.scalar.dma_start(out=bias_rows[P // 2 : P, :], in_=b_hh.rearrange("l d (r c) -> (l d r) c", c=P))
+        for l in range(LAYERS):
+            nc.vector.memset(w_planes[l][:].bitcast(I32), 0)
+        nc.vector.memset(warm_in[:], 0.0)
+        nc.scalar.activation(out=warm_out[:], in_=warm_in[:], func=SIGMOID)
+        make_identity(nc, identity[:])
+
+        def load_tokens(c):
+            rows = h_layer0[c * CHUNK : (c + 1) * CHUNK, :]
+            nc.sync.dma_start(out=x_rows[c][:], in_=rows.rearrange("(i p) f -> p i f", p=P))
+
+        def load_planes(l):
+            groups = w_ih_scales[4 * l : 4 * l + 4]
+            for quadrant in range(4):
+                nc.sync.dma_start(
+                    out=w_planes[l][32 * quadrant : 32 * quadrant + 16, :].bitcast(I32),
+                    in_=groups[:, 4 * quadrant : 4 * quadrant + 4, :].bitcast(I32),
+                )
+
+        def load_words(l, d):
+            for first_block, last_block in ((BLOCK_I, BLOCK_I), (BLOCK_G, BLOCK_O)):
+                some = slice(first_block * HIDDEN * PACK, (last_block + 1) * HIDDEN * PACK)
+                for k_pass in range(PASSES):
+                    e = (l * DIRECTIONS + d) * PASSES + k_pass
+                    nc.sync.dma_start(
+                        out=w_words[e][:, some].bitcast(I32),
+                        in_=w_ih_words[e].rearrange("p n t -> p (n t)")[:, some].bitcast(I32),
+                    )
+
+        load_tokens(0)
+        load_planes(0)
+        load_words(0, 0)
+        load_tokens(1)
+        load_words(0, 1)
+        load_planes(1)
+        load_words(1, 0)
+        load_words(1, 1)
+
+        nc.vector.tensor_copy(out=bias_rows_f32[:], in_=bias_rows[:])
+        bias_turned = turn_banks.tile([P, P], F32, tag="turned")
+        nc.tensor.transpose(bias_turned[:], bias_rows_f32[:], identity[:])
+        nc.vector.tensor_copy(out=bias_ih[:], in_=bias_turned[:, 0 : P // 2])
+        nc.vector.tensor_tensor(out=bias[:], in0=bias_ih[:], in1=bias_turned[:, P // 2 : P], op=ADD)
+
+        grouped_of = {}
+
+        def group_input(half):
+            layer, c, k_pass = half_place(half)
+            turned = turn_banks.tile([P, 2, CHUNK], F32, tag="turned")
+            for i in range(TOKEN_TILES):
+                pairs = x_rows[c][:, i, :].bitcast(F32)
+                for u in range(2):
+                    nc.tensor.transpose(
+                        turned[:, u, i * P : (i + 1) * P],
+                        pairs[:, k_pass * (K_PASS // 2) + u : (k_pass + 1) * (K_PASS // 2) : 2],
+                        identity[:],
+                    )
+            grouped = stage.tile([P, CHUNK, PACK], BF16, tag="grouped", align_bytes=64)
+            nc.vector.tensor_copy(out=grouped[:].bitcast(F32), in_=turned[:].rearrange("p u n -> p n u"))
+            grouped_of[half] = grouped
+
+        def group_parked(half):
+            layer, c, k_pass = half_place(half)
+            grouped = stage.tile([P, CHUNK, PACK], BF16, tag="grouped", align_bytes=64)
+            nc.vector.tensor_copy(out=grouped[:], in_=fetched_of[half][:].rearrange("p t n -> p n t"))
+            grouped_of[half] = grouped
+
+        def quantise(half):
+            nc.vector.quantize_mx(
+                out=h_words[:, half, :].bitcast(FP8X4),
+                scales=h_planes[:, half, :],
+                in_=grouped_of[half][:].rearrange("p n t -> p (n t)"),
+            )
+
+        banks_of = {}
+        acts_of = {}
+        h_of = {}
+        fetched_of = {}
+
+        def gate_group(acc, unit, block, j):
+            layer, c, d, pair = unit_place(unit)
+            first = block * HIDDEN + (pair * PAIR + j) * P
+            for k_pass in range(PASSES):
+                in_layer = d * PASSES + k_pass
+                half = (layer * CHUNKS + c) * PASSES + k_pass
+                nc.tensor.matmul_mx(
+                    out=acc,
+                    lhsT=w_words[layer * DIRECTIONS * PASSES + in_layer][:, first * PACK : (first + P) * PACK].bitcast(FP8X4),
+                    lhsT_scale=w_planes[layer][4 * in_layer : P, first : first + P],
+                    rhs=h_words[:, half, :].bitcast(FP8X4),
+                    rhs_scale=h_planes[:, half, :],
+                    start=(k_pass == 0),
+                    stop=(k_pass == PASSES - 1),
+                )
+
+        def multiply(unit):
+            ig = [gate_banks.tile([P, 2, CHUNK], F32, name="ig%d" % j, tag="ig%d" % j) for j in range(PAIR)]
+            oo = gate_banks.tile([P, PAIR, CHUNK], F32, tag="oo")
+            for j in range(PAIR):
+                gate_group(ig[j][:, 0, :], unit, BLOCK_I, j)
+                gate_group(ig[j][:, 1, :], unit, BLOCK_G, j)
+            for j in range(PAIR):
+                gate_group(oo[:, j, :], unit, BLOCK_O, j)
+            banks_of[unit] = (ig, oo)
+
+        def bias_column(unit, block, j):
+            layer, c, d, pair = unit_place(unit)
+            r = ((layer * DIRECTIONS + d) * GATE_BLOCKS + block) * TILES_PER_BLOCK + pair * PAIR + j
+            return bias[:, r : r + 1]
+
+        def gates(unit):
+            ig, oo = banks_of[unit]
+            ig_act = work.tile([P, PAIR, 2, CHUNK], F32, tag="ig_act")
+            o_act = work.tile([P, PAIR, CHUNK], F32, tag="o_act")
+            cell = work.tile([P, PAIR, CHUNK], F32, tag="cell")
+            for j in range(PAIR):
+                nc.scalar.activation(out=ig_act[:, j, 0, :], in_=ig[j][:, 0, :], func=SIGMOID, bias=bias_column(unit, BLOCK_I, j))
+                nc.scalar.activation(out=ig_act[:, j, 1, :], in_=ig[j][:, 1, :], func=TANH, bias=bias_column(unit, BLOCK_G, j))
+                nc.vector.tensor_tensor(out=cell[:, j, :], in0=ig_act[:, j, 0, :], in1=ig_act[:, j, 1, :], op=MULT)
+            for j in range(PAIR):
+                nc.scalar.activation(out=o_act[:, j, :], in_=oo[:, j, :], func=SIGMOID, bias=bias_column(unit, BLOCK_O, j))
+            acts_of[unit] = (o_act, cell)
+
+        def hidden(unit):
+            o_act, cell = acts_of[unit]
+            cell_act = work.tile([P, PAIR, CHUNK], F32, tag="cell_act")
+            h_turned = leave.tile([P, PAIR, CHUNK], F32, tag="h_turned")
+            nc.scalar.activation(out=cell_act[:], in_=cell[:], func=TANH)
+            nc.vector.tensor_tensor(out=h_turned[:], in0=o_act[:], in1=cell_act[:], op=MULT)
+            h_of[unit] = h_turned
+
+        def park(unit):
+            layer, c, d, pair = unit_place(unit)
+            first = d * HIDDEN + pair * PAIR * P
+            nc.sync.dma_start(
+                out=parked[c][first : first + PAIR * P, :].rearrange("(j p) n -> p j n", p=P), in_=h_of[unit][:]
+            )
+            if pair == PAIRS - 1:
+                half = (CHUNKS + c) * PASSES + d
+                fetched = stage.tile([P, PACK, CHUNK], F32, tag="fetched")
+                nc.sync.dma_start(
+                    out=fetched[:], in_=parked[c][d * K_PASS : (d + 1) * K_PASS, :].rearrange("(p t) n -> p t n", t=PACK)
+                )
+                fetched_of[half] = fetched
+
+        def deliver(unit):
+            layer, c, d, pair = unit_place(unit)
+            first = d * HIDDEN + pair * PAIR * P
+            h_rows = turn_banks.tile([P, TOKEN_TILES, PAIR, P], F32, tag="turned")
+            for i in range(TOKEN_TILES):
+                for j in range(PAIR):
+                    nc.tensor.transpose(h_rows[:, i, j, :], h_of[unit][:, j, i * P : (i + 1) * P], identity[:])
+            result = leave.tile([P, TOKEN_TILES, PAIR * P], F32, tag="result")
+            nc.vector.tensor_copy(out=result[:], in_=h_rows[:].rearrange("p i j f -> p i (j f)"))
+            nc.sync.dma_start(
+                out=out_rows[c * CHUNK : (c + 1) * CHUNK, first : first + PAIR * P].rearrange("(i p) f -> p i f", p=P),
+                in_=result[:],
+            )
+
+        for step in range(FIRST_STEP, UNITS):
+            half = (step - FIRST_STEP) // 2
+            makes_operand = (step - FIRST_STEP) % 2 == 0 and half < HALVES
+            if step >= 0:
+                gates(step)
+            if step - 1 >= UNITS_PER_LAYER:
+                deliver(step - 1)
+            if makes_operand and half < CHUNKS * PASSES:
+                group_input(half)
+            if makes_operand and half >= CHUNKS * PASSES:
+                group_parked(half)
+            if step >= 0:
+                hidden(step)
+            if 0 <= step < UNITS_PER_LAYER:
+                park(step)
+            if makes_operand:
+                quantise(half)
+            if 0 <= step + AHEAD < UNITS:
+                multiply(step + AHEAD)
+        deliver(UNITS - 1)

@@ -23,6 +23,7 @@ HIDDEN = 512
 LAYERS = 2
 DIRECTIONS = 2
 PASSES = FEATURES // K_PASS
+GROUPS_PER_LAYER = DIRECTIONS * PASSES
 GATE_BLOCKS = 4
 BLOCK_I, BLOCK_G, BLOCK_O = 0, 2, 3
 TILES_PER_BLOCK = HIDDEN // P
@@ -65,7 +66,8 @@ def tile_lstmnetwork_pb_e_kernel(tc, h_layer0, w_ih_words, w_ih_scales, b_ih, b_
     nc = tc.nc
     out_rows = out.rearrange("b c f -> (b c) f")
     parked = [
-        out_rows[c * CHUNK : (c + 1) * CHUNK, :].rearrange("r (a n) -> (r a) n", n=CHUNK) for c in range(CHUNKS)
+        out_rows.bitcast(BF16)[c * CHUNK : c * CHUNK + CHUNK // 2, :].rearrange("r (a n) -> (r a) n", n=CHUNK)
+        for c in range(CHUNKS)
     ]
 
     with ExitStack() as ctx:
@@ -113,24 +115,27 @@ def tile_lstmnetwork_pb_e_kernel(tc, h_layer0, w_ih_words, w_ih_scales, b_ih, b_
                     in_=groups[:, 4 * quadrant : 4 * quadrant + 4, :].bitcast(I32),
                 )
 
-        def load_words(l, d):
-            for first_block, last_block in ((BLOCK_I, BLOCK_I), (BLOCK_G, BLOCK_O)):
-                some = slice(first_block * HIDDEN * PACK, (last_block + 1) * HIDDEN * PACK)
+        def load_words(e, first_block, last_block):
+            some = slice(first_block * HIDDEN * PACK, (last_block + 1) * HIDDEN * PACK)
+            nc.sync.dma_start(
+                out=w_words[e][:, some].bitcast(I32),
+                in_=w_ih_words[e].rearrange("p n t -> p (n t)")[:, some].bitcast(I32),
+            )
+
+        def load_first_layer_words(d):
+            for block in (BLOCK_I, BLOCK_G, BLOCK_O):
                 for k_pass in range(PASSES):
-                    e = (l * DIRECTIONS + d) * PASSES + k_pass
-                    nc.sync.dma_start(
-                        out=w_words[e][:, some].bitcast(I32),
-                        in_=w_ih_words[e].rearrange("p n t -> p (n t)")[:, some].bitcast(I32),
-                    )
+                    load_words(d * PASSES + k_pass, block, block)
 
         load_tokens(0)
         load_planes(0)
-        load_words(0, 0)
+        load_first_layer_words(0)
         load_tokens(1)
-        load_words(0, 1)
+        load_first_layer_words(1)
         load_planes(1)
-        load_words(1, 0)
-        load_words(1, 1)
+        for e in range(GROUPS_PER_LAYER, 2 * GROUPS_PER_LAYER):
+            load_words(e, BLOCK_I, BLOCK_I)
+            load_words(e, BLOCK_G, BLOCK_O)
 
         nc.vector.tensor_copy(out=bias_rows_f32[:], in_=bias_rows[:])
         bias_turned = turn_banks.tile([P, P], F32, tag="turned")
@@ -152,7 +157,10 @@ def tile_lstmnetwork_pb_e_kernel(tc, h_layer0, w_ih_words, w_ih_scales, b_ih, b_
                         identity[:],
                     )
             grouped = stage.tile([P, CHUNK, PACK], BF16, tag="grouped", align_bytes=64)
-            nc.vector.tensor_copy(out=grouped[:].bitcast(F32), in_=turned[:].rearrange("p u n -> p n u"))
+            if c == 0:
+                nc.scalar.copy(out=grouped[:].bitcast(F32), in_=turned[:].rearrange("p u n -> p n u"))
+            else:
+                nc.vector.tensor_copy(out=grouped[:].bitcast(F32), in_=turned[:].rearrange("p u n -> p n u"))
             grouped_of[half] = grouped
 
         def group_parked(half):
@@ -169,8 +177,9 @@ def tile_lstmnetwork_pb_e_kernel(tc, h_layer0, w_ih_words, w_ih_scales, b_ih, b_
             )
 
         banks_of = {}
-        acts_of = {}
+        cell_of = {}
         h_of = {}
+        turned_of = {}
         fetched_of = {}
 
         def gate_group(acc, unit, block, j):
@@ -204,26 +213,25 @@ def tile_lstmnetwork_pb_e_kernel(tc, h_layer0, w_ih_words, w_ih_scales, b_ih, b_
             r = ((layer * DIRECTIONS + d) * GATE_BLOCKS + block) * TILES_PER_BLOCK + pair * PAIR + j
             return bias[:, r : r + 1]
 
-        def gates(unit):
+        def cell_state(unit, j):
             ig, oo = banks_of[unit]
-            ig_act = work.tile([P, PAIR, 2, CHUNK], F32, tag="ig_act")
-            o_act = work.tile([P, PAIR, CHUNK], F32, tag="o_act")
-            cell = work.tile([P, PAIR, CHUNK], F32, tag="cell")
-            for j in range(PAIR):
-                nc.scalar.activation(out=ig_act[:, j, 0, :], in_=ig[j][:, 0, :], func=SIGMOID, bias=bias_column(unit, BLOCK_I, j))
-                nc.scalar.activation(out=ig_act[:, j, 1, :], in_=ig[j][:, 1, :], func=TANH, bias=bias_column(unit, BLOCK_G, j))
-                nc.vector.tensor_tensor(out=cell[:, j, :], in0=ig_act[:, j, 0, :], in1=ig_act[:, j, 1, :], op=MULT)
-            for j in range(PAIR):
-                nc.scalar.activation(out=o_act[:, j, :], in_=oo[:, j, :], func=SIGMOID, bias=bias_column(unit, BLOCK_O, j))
-            acts_of[unit] = (o_act, cell)
+            ig_act = work.tile([P, 2, CHUNK], F32, tag="ig_act%d" % j)
+            cell = work.tile([P, CHUNK], F32, tag="cell%d" % j)
+            nc.scalar.activation(out=ig_act[:, 0, :], in_=ig[j][:, 0, :], func=SIGMOID, bias=bias_column(unit, BLOCK_I, j))
+            nc.scalar.activation(out=ig_act[:, 1, :], in_=ig[j][:, 1, :], func=TANH, bias=bias_column(unit, BLOCK_G, j))
+            nc.vector.tensor_tensor(out=cell[:], in0=ig_act[:, 0, :], in1=ig_act[:, 1, :], op=MULT)
+            cell_of[unit, j] = cell
 
-        def hidden(unit):
-            o_act, cell = acts_of[unit]
-            cell_act = work.tile([P, PAIR, CHUNK], F32, tag="cell_act")
-            h_turned = leave.tile([P, PAIR, CHUNK], F32, tag="h_turned")
-            nc.scalar.activation(out=cell_act[:], in_=cell[:], func=TANH)
-            nc.vector.tensor_tensor(out=h_turned[:], in0=o_act[:], in1=cell_act[:], op=MULT)
-            h_of[unit] = h_turned
+        def hidden(unit, j):
+            ig, oo = banks_of[unit]
+            if j == 0 and unit < UNITS_PER_LAYER:
+                h_of[unit] = leave.tile([P, PAIR, CHUNK], BF16, name="h_parked", tag="h_parked")
+            if j == 0 and unit >= UNITS_PER_LAYER:
+                h_of[unit] = leave.tile([P, PAIR, CHUNK], F32, name="h_last", tag="h_last")
+            oc_act = work.tile([P, 2, CHUNK], F32, tag="oc_act%d" % j)
+            nc.scalar.activation(out=oc_act[:, 0, :], in_=oo[:, j, :], func=SIGMOID, bias=bias_column(unit, BLOCK_O, j))
+            nc.scalar.activation(out=oc_act[:, 1, :], in_=cell_of[unit, j][:], func=TANH)
+            nc.vector.tensor_tensor(out=h_of[unit][:, j, :], in0=oc_act[:, 0, :], in1=oc_act[:, 1, :], op=MULT)
 
         def park(unit):
             layer, c, d, pair = unit_place(unit)
@@ -233,43 +241,51 @@ def tile_lstmnetwork_pb_e_kernel(tc, h_layer0, w_ih_words, w_ih_scales, b_ih, b_
             )
             if pair == PAIRS - 1:
                 half = (CHUNKS + c) * PASSES + d
-                fetched = stage.tile([P, PACK, CHUNK], F32, tag="fetched")
+                fetched = stage.tile([P, PACK, CHUNK], BF16, tag="fetched")
                 nc.sync.dma_start(
                     out=fetched[:], in_=parked[c][d * K_PASS : (d + 1) * K_PASS, :].rearrange("(p t) n -> p t n", t=PACK)
                 )
                 fetched_of[half] = fetched
 
-        def deliver(unit):
-            layer, c, d, pair = unit_place(unit)
-            first = d * HIDDEN + pair * PAIR * P
+        def turn(unit):
             h_rows = turn_banks.tile([P, TOKEN_TILES, PAIR, P], F32, tag="turned")
             for i in range(TOKEN_TILES):
                 for j in range(PAIR):
                     nc.tensor.transpose(h_rows[:, i, j, :], h_of[unit][:, j, i * P : (i + 1) * P], identity[:])
+            turned_of[unit] = h_rows
+
+        def store_rows(unit):
+            layer, c, d, pair = unit_place(unit)
+            first = d * HIDDEN + pair * PAIR * P
             result = leave.tile([P, TOKEN_TILES, PAIR * P], F32, tag="result")
-            nc.vector.tensor_copy(out=result[:], in_=h_rows[:].rearrange("p i j f -> p i (j f)"))
+            nc.vector.tensor_copy(out=result[:], in_=turned_of[unit][:].rearrange("p i j f -> p i (j f)"))
             nc.sync.dma_start(
                 out=out_rows[c * CHUNK : (c + 1) * CHUNK, first : first + PAIR * P].rearrange("(i p) f -> p i f", p=P),
                 in_=result[:],
             )
 
-        for step in range(FIRST_STEP, UNITS):
+        for step in range(FIRST_STEP, UNITS + 2):
             half = (step - FIRST_STEP) // 2
             makes_operand = (step - FIRST_STEP) % 2 == 0 and half < HALVES
-            if step >= 0:
-                gates(step)
-            if step - 1 >= UNITS_PER_LAYER:
-                deliver(step - 1)
+            if 0 <= step < UNITS:
+                cell_state(step, 0)
+            if UNITS_PER_LAYER <= step - 2:
+                store_rows(step - 2)
+            if 0 <= step - 1 < UNITS:
+                hidden(step - 1, 1)
+            if 0 <= step - 1 < UNITS_PER_LAYER:
+                park(step - 1)
+            if UNITS_PER_LAYER <= step - 1 < UNITS:
+                turn(step - 1)
+            if 0 <= step < UNITS:
+                cell_state(step, 1)
             if makes_operand and half < CHUNKS * PASSES:
                 group_input(half)
             if makes_operand and half >= CHUNKS * PASSES:
                 group_parked(half)
-            if step >= 0:
-                hidden(step)
-            if 0 <= step < UNITS_PER_LAYER:
-                park(step)
             if makes_operand:
                 quantise(half)
+            if 0 <= step < UNITS:
+                hidden(step, 0)
             if 0 <= step + AHEAD < UNITS:
                 multiply(step + AHEAD)
-        deliver(UNITS - 1)

@@ -37,7 +37,8 @@ UNITS_PER_LAYER = CHUNKS * UNITS_PER_CHUNK
 UNITS = LAYERS * UNITS_PER_LAYER
 AHEAD = 2
 HALVES = LAYERS * CHUNKS * PASSES
-FIRST_STEP = -2 * AHEAD
+WARM_BEFORE = 5
+WARM_AFTER = 2
 
 FLOPS = 2 * TOKENS * FEATURES * 3 * HIDDEN * LAYERS * DIRECTIONS
 BYTES = (
@@ -92,11 +93,13 @@ def tile_lstmnetwork_pb_e_kernel(tc, h_layer0, w_ih_words, w_ih_scales, b_ih, b_
         bias_rows_f32 = keep.tile([P, P], F32)
         bias_ih = keep.tile([P, P // 2], F32)
         bias = keep.tile([P, P // 2], F32)
+        zeros = keep.tile([P, HIDDEN], BF16)
         warm_in = keep.tile([P, 1], F32)
         warm_out = keep.tile([P, 1], F32)
 
         nc.scalar.dma_start(out=bias_rows[0 : P // 2, :], in_=b_ih.rearrange("l d (r c) -> (l d r) c", c=P))
         nc.scalar.dma_start(out=bias_rows[P // 2 : P, :], in_=b_hh.rearrange("l d (r c) -> (l d r) c", c=P))
+        nc.vector.memset(zeros[:], 0.0)
         for l in range(LAYERS):
             nc.vector.memset(w_planes[l][:].bitcast(I32), 0)
         nc.vector.memset(warm_in[:], 0.0)
@@ -136,6 +139,13 @@ def tile_lstmnetwork_pb_e_kernel(tc, h_layer0, w_ih_words, w_ih_scales, b_ih, b_
         for e in range(GROUPS_PER_LAYER, 2 * GROUPS_PER_LAYER):
             load_words(e, BLOCK_I, BLOCK_I)
             load_words(e, BLOCK_G, BLOCK_O)
+
+        def keep_tensor_engine_busy(products):
+            idle = turn_banks.tile([P, HIDDEN], F32, tag="turned")
+            for n in range(products):
+                nc.tensor.matmul(idle[:], lhsT=zeros[:, 0:P], rhs=zeros[:], start=(n == 0), stop=(n == products - 1))
+
+        keep_tensor_engine_busy(WARM_BEFORE)
 
         nc.vector.tensor_copy(out=bias_rows_f32[:], in_=bias_rows[:])
         bias_turned = turn_banks.tile([P, P], F32, tag="turned")
@@ -249,8 +259,8 @@ def tile_lstmnetwork_pb_e_kernel(tc, h_layer0, w_ih_words, w_ih_scales, b_ih, b_
 
         def turn(unit):
             h_rows = turn_banks.tile([P, TOKEN_TILES, PAIR, P], F32, tag="turned")
-            for i in range(TOKEN_TILES):
-                for j in range(PAIR):
+            for j in range(PAIR):
+                for i in range(TOKEN_TILES):
                     nc.tensor.transpose(h_rows[:, i, j, :], h_of[unit][:, j, i * P : (i + 1) * P], identity[:])
             turned_of[unit] = h_rows
 
@@ -264,10 +274,17 @@ def tile_lstmnetwork_pb_e_kernel(tc, h_layer0, w_ih_words, w_ih_scales, b_ih, b_
                 in_=result[:],
             )
 
-        for step in range(FIRST_STEP, UNITS + 2):
-            half = (step - FIRST_STEP) // 2
-            makes_operand = (step - FIRST_STEP) % 2 == 0 and half < HALVES
-            if 0 <= step < UNITS:
+        for half in range(PASSES):
+            group_input(half)
+        keep_tensor_engine_busy(WARM_AFTER)
+        for half in range(PASSES):
+            quantise(half)
+        for unit in range(AHEAD):
+            multiply(unit)
+        for step in range(UNITS + 2):
+            half = PASSES + step // 2
+            makes_operand = step % 2 == 0 and half < HALVES
+            if step < UNITS:
                 cell_state(step, 0)
             if UNITS_PER_LAYER <= step - 2:
                 store_rows(step - 2)
@@ -277,7 +294,7 @@ def tile_lstmnetwork_pb_e_kernel(tc, h_layer0, w_ih_words, w_ih_scales, b_ih, b_
                 park(step - 1)
             if UNITS_PER_LAYER <= step - 1 < UNITS:
                 turn(step - 1)
-            if 0 <= step < UNITS:
+            if step < UNITS:
                 cell_state(step, 1)
             if makes_operand and half < CHUNKS * PASSES:
                 group_input(half)
@@ -285,7 +302,7 @@ def tile_lstmnetwork_pb_e_kernel(tc, h_layer0, w_ih_words, w_ih_scales, b_ih, b_
                 group_parked(half)
             if makes_operand:
                 quantise(half)
-            if 0 <= step < UNITS:
+            if step < UNITS:
                 hidden(step, 0)
-            if 0 <= step + AHEAD < UNITS:
+            if step + AHEAD < UNITS:
                 multiply(step + AHEAD)

@@ -37,8 +37,6 @@ UNITS_PER_LAYER = CHUNKS * UNITS_PER_CHUNK
 UNITS = LAYERS * UNITS_PER_LAYER
 AHEAD = 2
 HALVES = LAYERS * CHUNKS * PASSES
-WARM_BEFORE = 5
-WARM_AFTER = 2
 
 FLOPS = 2 * TOKENS * FEATURES * 3 * HIDDEN * LAYERS * DIRECTIONS
 BYTES = (
@@ -93,13 +91,12 @@ def tile_lstmnetwork_pb_e_kernel(tc, h_layer0, w_ih_words, w_ih_scales, b_ih, b_
         bias_rows_f32 = keep.tile([P, P], F32)
         bias_ih = keep.tile([P, P // 2], F32)
         bias = keep.tile([P, P // 2], F32)
-        zeros = keep.tile([P, HIDDEN], BF16)
+        pace = keep.tile([P, GROUPS_PER_LAYER], BF16)
         warm_in = keep.tile([P, 1], F32)
         warm_out = keep.tile([P, 1], F32)
 
         nc.scalar.dma_start(out=bias_rows[0 : P // 2, :], in_=b_ih.rearrange("l d (r c) -> (l d r) c", c=P))
         nc.scalar.dma_start(out=bias_rows[P // 2 : P, :], in_=b_hh.rearrange("l d (r c) -> (l d r) c", c=P))
-        nc.vector.memset(zeros[:], 0.0)
         for l in range(LAYERS):
             nc.vector.memset(w_planes[l][:].bitcast(I32), 0)
         nc.vector.memset(warm_in[:], 0.0)
@@ -118,17 +115,22 @@ def tile_lstmnetwork_pb_e_kernel(tc, h_layer0, w_ih_words, w_ih_scales, b_ih, b_
                     in_=groups[:, 4 * quadrant : 4 * quadrant + 4, :].bitcast(I32),
                 )
 
-        def load_words(e, first_block, last_block):
-            some = slice(first_block * HIDDEN * PACK, (last_block + 1) * HIDDEN * PACK)
-            nc.sync.dma_start(
-                out=w_words[e][:, some].bitcast(I32),
-                in_=w_ih_words[e].rearrange("p n t -> p (n t)")[:, some].bitcast(I32),
-            )
+        def word_bytes(e, first, columns):
+            some = slice(first * PACK, (first + columns) * PACK)
+            return w_words[e][:, some], w_ih_words[e].rearrange("p n t -> p (n t)")[:, some]
 
         def load_first_layer_words(d):
-            for block in (BLOCK_I, BLOCK_G, BLOCK_O):
-                for k_pass in range(PASSES):
-                    load_words(d * PASSES + k_pass, block, block)
+            for pair in range(PAIRS):
+                for block in (BLOCK_I, BLOCK_G, BLOCK_O):
+                    for k_pass in range(PASSES):
+                        in_sbuf, in_hbm = word_bytes(d * PASSES + k_pass, block * HIDDEN + pair * PAIR * P, PAIR * P)
+                        nc.sync.dma_start(out=in_sbuf.bitcast(I32), in_=in_hbm.bitcast(I32))
+
+        def load_second_layer_words(in_layer, after):
+            nc.gpsimd.tensor_copy(out=pace[:, in_layer : in_layer + 1], in_=after)
+            for first_block, blocks in ((BLOCK_I, 1), (BLOCK_G, 2)):
+                in_sbuf, in_hbm = word_bytes(GROUPS_PER_LAYER + in_layer, first_block * HIDDEN, blocks * HIDDEN)
+                nc.gpsimd.dma_start(out=in_sbuf.bitcast(F32), in_=in_hbm.bitcast(F32))
 
         load_tokens(0)
         load_planes(0)
@@ -136,16 +138,6 @@ def tile_lstmnetwork_pb_e_kernel(tc, h_layer0, w_ih_words, w_ih_scales, b_ih, b_
         load_tokens(1)
         load_first_layer_words(1)
         load_planes(1)
-        for e in range(GROUPS_PER_LAYER, 2 * GROUPS_PER_LAYER):
-            load_words(e, BLOCK_I, BLOCK_I)
-            load_words(e, BLOCK_G, BLOCK_O)
-
-        def keep_tensor_engine_busy(products):
-            idle = turn_banks.tile([P, HIDDEN], F32, tag="turned")
-            for n in range(products):
-                nc.tensor.matmul(idle[:], lhsT=zeros[:, 0:P], rhs=zeros[:], start=(n == 0), stop=(n == products - 1))
-
-        keep_tensor_engine_busy(WARM_BEFORE)
 
         nc.vector.tensor_copy(out=bias_rows_f32[:], in_=bias_rows[:])
         bias_turned = turn_banks.tile([P, P], F32, tag="turned")
@@ -276,7 +268,6 @@ def tile_lstmnetwork_pb_e_kernel(tc, h_layer0, w_ih_words, w_ih_scales, b_ih, b_
 
         for half in range(PASSES):
             group_input(half)
-        keep_tensor_engine_busy(WARM_AFTER)
         for half in range(PASSES):
             quantise(half)
         for unit in range(AHEAD):
@@ -304,5 +295,7 @@ def tile_lstmnetwork_pb_e_kernel(tc, h_layer0, w_ih_words, w_ih_scales, b_ih, b_
                 quantise(half)
             if step < UNITS:
                 hidden(step, 0)
+            if 1 <= step <= GROUPS_PER_LAYER:
+                load_second_layer_words(step - 1, h_of[step][:, 0, 0:1])
             if step + AHEAD < UNITS:
                 multiply(step + AHEAD)

@@ -64,11 +64,6 @@ def half_place(half):
 def tile_lstmnetwork_pb_e_kernel(tc, h_layer0, w_ih_words, w_ih_scales, b_ih, b_hh, out):
     nc = tc.nc
     out_rows = out.rearrange("b c f -> (b c) f")
-    parked = [
-        out_rows.bitcast(BF16)[c * CHUNK : c * CHUNK + CHUNK // 2, :].rearrange("r (a n) -> (r a) n", n=CHUNK)
-        for c in range(CHUNKS)
-    ]
-
     with ExitStack() as ctx:
         ctx.enter_context(tc.manual_schedule())
         keep = ctx.enter_context(tc.tile_pool(name="keep", bufs=1))
@@ -91,7 +86,6 @@ def tile_lstmnetwork_pb_e_kernel(tc, h_layer0, w_ih_words, w_ih_scales, b_ih, b_
         bias_rows_f32 = keep.tile([P, P], F32)
         bias_ih = keep.tile([P, P // 2], F32)
         bias = keep.tile([P, P // 2], F32)
-        pace = keep.tile([P, GROUPS_PER_LAYER], BF16)
         warm_in = keep.tile([P, 1], F32)
         warm_out = keep.tile([P, 1], F32)
 
@@ -104,8 +98,10 @@ def tile_lstmnetwork_pb_e_kernel(tc, h_layer0, w_ih_words, w_ih_scales, b_ih, b_
         make_identity(nc, identity[:])
 
         def load_tokens(c):
-            rows = h_layer0[c * CHUNK : (c + 1) * CHUNK, :]
-            nc.sync.dma_start(out=x_rows[c][:], in_=rows.rearrange("(i p) f -> p i f", p=P))
+            rows = h_layer0[c * CHUNK : (c + 1) * CHUNK, :].rearrange("(i p) f -> p i f", p=P)
+            for k_pass in range(PASSES):
+                some = slice(k_pass * K_PASS, (k_pass + 1) * K_PASS)
+                nc.sync.dma_start(out=x_rows[c][:, :, some], in_=rows[:, :, some])
 
         def load_planes(l):
             groups = w_ih_scales[4 * l : 4 * l + 4]
@@ -126,11 +122,12 @@ def tile_lstmnetwork_pb_e_kernel(tc, h_layer0, w_ih_words, w_ih_scales, b_ih, b_
                         in_sbuf, in_hbm = word_bytes(d * PASSES + k_pass, block * HIDDEN + pair * PAIR * P, PAIR * P)
                         nc.sync.dma_start(out=in_sbuf.bitcast(I32), in_=in_hbm.bitcast(I32))
 
-        def load_second_layer_words(in_layer, after):
-            nc.gpsimd.tensor_copy(out=pace[:, in_layer : in_layer + 1], in_=after)
+        def load_second_layer_words(d):
             for first_block, blocks in ((BLOCK_I, 1), (BLOCK_G, 2)):
-                in_sbuf, in_hbm = word_bytes(GROUPS_PER_LAYER + in_layer, first_block * HIDDEN, blocks * HIDDEN)
-                nc.gpsimd.dma_start(out=in_sbuf.bitcast(F32), in_=in_hbm.bitcast(F32))
+                for k_pass in range(PASSES):
+                    e = GROUPS_PER_LAYER + d * PASSES + k_pass
+                    in_sbuf, in_hbm = word_bytes(e, first_block * HIDDEN, blocks * HIDDEN)
+                    nc.sync.dma_start(out=in_sbuf.bitcast(I32), in_=in_hbm.bitcast(I32))
 
         load_tokens(0)
         load_planes(0)
@@ -138,6 +135,8 @@ def tile_lstmnetwork_pb_e_kernel(tc, h_layer0, w_ih_words, w_ih_scales, b_ih, b_
         load_tokens(1)
         load_first_layer_words(1)
         load_planes(1)
+        load_second_layer_words(0)
+        load_second_layer_words(1)
 
         nc.vector.tensor_copy(out=bias_rows_f32[:], in_=bias_rows[:])
         bias_turned = turn_banks.tile([P, P], F32, tag="turned")
@@ -227,7 +226,7 @@ def tile_lstmnetwork_pb_e_kernel(tc, h_layer0, w_ih_words, w_ih_scales, b_ih, b_
         def hidden(unit, j):
             ig, oo = banks_of[unit]
             if j == 0 and unit < UNITS_PER_LAYER:
-                h_of[unit] = leave.tile([P, PAIR, CHUNK], BF16, name="h_parked", tag="h_parked")
+                h_of[unit] = leave.tile([P, PAIR, CHUNK], BF16, name="h_first", tag="h_first")
             if j == 0 and unit >= UNITS_PER_LAYER:
                 h_of[unit] = leave.tile([P, PAIR, CHUNK], F32, name="h_last", tag="h_last")
             oc_act = work.tile([P, 2, CHUNK], F32, tag="oc_act%d" % j)
@@ -235,19 +234,13 @@ def tile_lstmnetwork_pb_e_kernel(tc, h_layer0, w_ih_words, w_ih_scales, b_ih, b_
             nc.scalar.activation(out=oc_act[:, 1, :], in_=cell_of[unit, j][:], func=TANH)
             nc.vector.tensor_tensor(out=h_of[unit][:, j, :], in0=oc_act[:, 0, :], in1=oc_act[:, 1, :], op=MULT)
 
-        def park(unit):
+        def hand_over(unit, j):
             layer, c, d, pair = unit_place(unit)
-            first = d * HIDDEN + pair * PAIR * P
-            nc.sync.dma_start(
-                out=parked[c][first : first + PAIR * P, :].rearrange("(j p) n -> p j n", p=P), in_=h_of[unit][:]
-            )
-            if pair == PAIRS - 1:
-                half = (CHUNKS + c) * PASSES + d
-                fetched = stage.tile([P, PACK, CHUNK], BF16, tag="fetched")
-                nc.sync.dma_start(
-                    out=fetched[:], in_=parked[c][d * K_PASS : (d + 1) * K_PASS, :].rearrange("(p t) n -> p t n", t=PACK)
-                )
-                fetched_of[half] = fetched
+            half = (CHUNKS + c) * PASSES + d
+            if pair == 0 and j == 0:
+                fetched_of[half] = stage.tile([P, PACK, CHUNK], BF16, name="fetched", tag="fetched", bufs=3)
+            first = (pair * PAIR + j) * (P // PACK)
+            nc.sync.dma_start(out=fetched_of[half][first : first + P // PACK, :, :], in_=h_of[unit][:, j, :])
 
         def turn(unit):
             h_rows = turn_banks.tile([P, TOKEN_TILES, PAIR, P], F32, tag="turned")
@@ -273,8 +266,9 @@ def tile_lstmnetwork_pb_e_kernel(tc, h_layer0, w_ih_words, w_ih_scales, b_ih, b_
         for unit in range(AHEAD):
             multiply(unit)
         for step in range(UNITS + 2):
-            half = PASSES + step // 2
-            makes_operand = step % 2 == 0 and half < HALVES
+            phase, k_pass = divmod(step + AHEAD + 1, UNITS_PER_CHUNK)
+            half = phase * PASSES + k_pass
+            makes_operand = k_pass < PASSES and half < HALVES
             if step < UNITS:
                 cell_state(step, 0)
             if UNITS_PER_LAYER <= step - 2:
@@ -282,7 +276,7 @@ def tile_lstmnetwork_pb_e_kernel(tc, h_layer0, w_ih_words, w_ih_scales, b_ih, b_
             if 0 <= step - 1 < UNITS:
                 hidden(step - 1, 1)
             if 0 <= step - 1 < UNITS_PER_LAYER:
-                park(step - 1)
+                hand_over(step - 1, 1)
             if UNITS_PER_LAYER <= step - 1 < UNITS:
                 turn(step - 1)
             if step < UNITS:
@@ -295,7 +289,7 @@ def tile_lstmnetwork_pb_e_kernel(tc, h_layer0, w_ih_words, w_ih_scales, b_ih, b_
                 quantise(half)
             if step < UNITS:
                 hidden(step, 0)
-            if 1 <= step <= GROUPS_PER_LAYER:
-                load_second_layer_words(step - 1, h_of[step][:, 0, 0:1])
+            if step < UNITS_PER_LAYER:
+                hand_over(step, 0)
             if step + AHEAD < UNITS:
                 multiply(step + AHEAD)

@@ -136,7 +136,6 @@ def tile_lstmnetwork_pb_e_kernel(tc, h_layer0, w_ih_words, w_ih_scales, b_ih, b_
         load_first_layer_words(1)
         load_planes(1)
         load_second_layer_words(0)
-        load_second_layer_words(1)
 
         nc.vector.tensor_copy(out=bias_rows_f32[:], in_=bias_rows[:])
         bias_turned = turn_banks.tile([P, P], F32, tag="turned")
@@ -226,7 +225,7 @@ def tile_lstmnetwork_pb_e_kernel(tc, h_layer0, w_ih_words, w_ih_scales, b_ih, b_
         def hidden(unit, j):
             ig, oo = banks_of[unit]
             if j == 0 and unit < UNITS_PER_LAYER:
-                h_of[unit] = leave.tile([P, PAIR, CHUNK], BF16, name="h_first", tag="h_first")
+                h_of[unit] = keep.tile([P, PAIR, CHUNK], BF16, name="h_first%d" % unit)
             if j == 0 and unit >= UNITS_PER_LAYER:
                 h_of[unit] = leave.tile([P, PAIR, CHUNK], F32, name="h_last", tag="h_last")
             oc_act = work.tile([P, 2, CHUNK], F32, tag="oc_act%d" % j)
@@ -277,6 +276,8 @@ def tile_lstmnetwork_pb_e_kernel(tc, h_layer0, w_ih_words, w_ih_scales, b_ih, b_
                 hidden(step - 1, 1)
             if 0 <= step - 1 < UNITS_PER_LAYER:
                 hand_over(step - 1, 1)
+            if step == UNITS_PER_CHUNK:
+                load_second_layer_words(1)
             if UNITS_PER_LAYER <= step - 1 < UNITS:
                 turn(step - 1)
             if step < UNITS:

@@ -91,9 +91,8 @@ def tile_lstmnetwork_pb_e_kernel(tc, h_layer0, w_ih_words, w_ih_scales, b_ih, b_
 
         nc.scalar.dma_start(out=bias_rows[0 : P // 2, :], in_=b_ih.rearrange("l d (r c) -> (l d r) c", c=P))
         nc.scalar.dma_start(out=bias_rows[P // 2 : P, :], in_=b_hh.rearrange("l d (r c) -> (l d r) c", c=P))
-        for l in range(LAYERS):
-            nc.vector.memset(w_planes[l][:].bitcast(I32), 0)
         nc.vector.memset(warm_in[:], 0.0)
+        nc.vector.memset(w_planes[1][:].bitcast(I32), 0)
         nc.scalar.activation(out=warm_out[:], in_=warm_in[:], func=SIGMOID)
         make_identity(nc, identity[:])
 
@@ -104,10 +103,10 @@ def tile_lstmnetwork_pb_e_kernel(tc, h_layer0, w_ih_words, w_ih_scales, b_ih, b_
                 nc.sync.dma_start(out=x_rows[c][:, :, some], in_=rows[:, :, some])
 
         def load_planes(l):
-            groups = w_ih_scales[4 * l : 4 * l + 4]
+            groups = w_ih_scales[4 * l : 8]
             for quadrant in range(4):
                 nc.sync.dma_start(
-                    out=w_planes[l][32 * quadrant : 32 * quadrant + 16, :].bitcast(I32),
+                    out=w_planes[l][32 * quadrant : 32 * quadrant + 32 - 16 * l, :].bitcast(I32),
                     in_=groups[:, 4 * quadrant : 4 * quadrant + 4, :].bitcast(I32),
                 )
 
@@ -129,19 +128,13 @@ def tile_lstmnetwork_pb_e_kernel(tc, h_layer0, w_ih_words, w_ih_scales, b_ih, b_
                     in_sbuf, in_hbm = word_bytes(e, first_block * HIDDEN, blocks * HIDDEN)
                     nc.sync.dma_start(out=in_sbuf.bitcast(I32), in_=in_hbm.bitcast(I32))
 
-        load_tokens(0)
         load_planes(0)
+        load_tokens(0)
         load_first_layer_words(0)
         load_tokens(1)
         load_first_layer_words(1)
         load_planes(1)
         load_second_layer_words(0)
-
-        nc.vector.tensor_copy(out=bias_rows_f32[:], in_=bias_rows[:])
-        bias_turned = turn_banks.tile([P, P], F32, tag="turned")
-        nc.tensor.transpose(bias_turned[:], bias_rows_f32[:], identity[:])
-        nc.vector.tensor_copy(out=bias_ih[:], in_=bias_turned[:, 0 : P // 2])
-        nc.vector.tensor_tensor(out=bias[:], in0=bias_ih[:], in1=bias_turned[:, P // 2 : P], op=ADD)
 
         grouped_of = {}
 
@@ -175,6 +168,13 @@ def tile_lstmnetwork_pb_e_kernel(tc, h_layer0, w_ih_words, w_ih_scales, b_ih, b_
                 scales=h_planes[:, half, :],
                 in_=grouped_of[half][:].rearrange("p n t -> p (n t)"),
             )
+
+        def spread_biases():
+            nc.vector.tensor_copy(out=bias_rows_f32[:], in_=bias_rows[:])
+            bias_turned = turn_banks.tile([P, P], F32, tag="turned")
+            nc.tensor.transpose(bias_turned[:], bias_rows_f32[:], identity[:])
+            nc.vector.tensor_copy(out=bias_ih[:], in_=bias_turned[:, 0 : P // 2])
+            nc.vector.tensor_tensor(out=bias[:], in0=bias_ih[:], in1=bias_turned[:, P // 2 : P], op=ADD)
 
         banks_of = {}
         cell_of = {}
@@ -241,20 +241,20 @@ def tile_lstmnetwork_pb_e_kernel(tc, h_layer0, w_ih_words, w_ih_scales, b_ih, b_
             first = (pair * PAIR + j) * (P // PACK)
             nc.sync.dma_start(out=fetched_of[half][first : first + P // PACK, :, :], in_=h_of[unit][:, j, :])
 
-        def turn(unit):
-            h_rows = turn_banks.tile([P, TOKEN_TILES, PAIR, P], F32, tag="turned")
-            for j in range(PAIR):
+        def turn(unit, first_tile=0, tiles=PAIR):
+            h_rows = turn_banks.tile([P, TOKEN_TILES, tiles, P], F32, tag="turned")
+            for j in range(tiles):
                 for i in range(TOKEN_TILES):
-                    nc.tensor.transpose(h_rows[:, i, j, :], h_of[unit][:, j, i * P : (i + 1) * P], identity[:])
+                    nc.tensor.transpose(h_rows[:, i, j, :], h_of[unit][:, first_tile + j, i * P : (i + 1) * P], identity[:])
             turned_of[unit] = h_rows
 
-        def store_rows(unit):
+        def store_rows(unit, first_tile=0, tiles=PAIR):
             layer, c, d, pair = unit_place(unit)
-            first = d * HIDDEN + pair * PAIR * P
-            result = leave.tile([P, TOKEN_TILES, PAIR * P], F32, tag="result")
+            first = d * HIDDEN + (pair * PAIR + first_tile) * P
+            result = leave.tile([P, TOKEN_TILES, tiles * P], F32, tag="result")
             nc.vector.tensor_copy(out=result[:], in_=turned_of[unit][:].rearrange("p i j f -> p i (j f)"))
             nc.sync.dma_start(
-                out=out_rows[c * CHUNK : (c + 1) * CHUNK, first : first + PAIR * P].rearrange("(i p) f -> p i f", p=P),
+                out=out_rows[c * CHUNK : (c + 1) * CHUNK, first : first + tiles * P].rearrange("(i p) f -> p i f", p=P),
                 in_=result[:],
             )
 
@@ -262,15 +262,16 @@ def tile_lstmnetwork_pb_e_kernel(tc, h_layer0, w_ih_words, w_ih_scales, b_ih, b_
             group_input(half)
         for half in range(PASSES):
             quantise(half)
+        spread_biases()
         for unit in range(AHEAD):
             multiply(unit)
-        for step in range(UNITS + 2):
+        for step in range(UNITS + 1):
             phase, k_pass = divmod(step + AHEAD + 1, UNITS_PER_CHUNK)
             half = phase * PASSES + k_pass
             makes_operand = k_pass < PASSES and half < HALVES
             if step < UNITS:
                 cell_state(step, 0)
-            if UNITS_PER_LAYER <= step - 2:
+            if UNITS_PER_LAYER <= step - 2 < UNITS - 2:
                 store_rows(step - 2)
             if 0 <= step - 1 < UNITS:
                 hidden(step - 1, 1)
@@ -278,10 +279,16 @@ def tile_lstmnetwork_pb_e_kernel(tc, h_layer0, w_ih_words, w_ih_scales, b_ih, b_
                 hand_over(step - 1, 1)
             if step == UNITS_PER_CHUNK:
                 load_second_layer_words(1)
-            if UNITS_PER_LAYER <= step - 1 < UNITS:
+            if UNITS_PER_LAYER <= step - 1 < UNITS - 1:
                 turn(step - 1)
+            if step == UNITS:
+                store_rows(UNITS - 1, 0, 1)
+                turn(UNITS - 1, 1, 1)
+                store_rows(UNITS - 1, 1, 1)
             if step < UNITS:
                 cell_state(step, 1)
+            if step == UNITS - 1:
+                store_rows(step - 1)
             if makes_operand and half < CHUNKS * PASSES:
                 group_input(half)
             if makes_operand and half >= CHUNKS * PASSES:
@@ -290,6 +297,8 @@ def tile_lstmnetwork_pb_e_kernel(tc, h_layer0, w_ih_words, w_ih_scales, b_ih, b_
                 quantise(half)
             if step < UNITS:
                 hidden(step, 0)
+            if step == UNITS - 1:
+                turn(step, 0, 1)
             if step < UNITS_PER_LAYER:
                 hand_over(step, 0)
             if step + AHEAD < UNITS:

@@ -75,8 +75,8 @@ def tile_lstmnetwork_pb_e_kernel(tc, h_layer0, w_ih_words, w_ih_scales, b_ih, b_
 
         x_rows = [keep.tile([P, TOKEN_TILES, FEATURES], BF16, name="x_rows%d" % c) for c in range(CHUNKS)]
         w_words = [
-            keep.tile([P, GATE_BLOCKS * HIDDEN * PACK], U8, name="w_words%d" % e, align_bytes=64)
-            for e in range(LAYERS * DIRECTIONS * PASSES)
+            keep.tile([P, PASSES, GATE_BLOCKS * HIDDEN * PACK], U8, name="w_words%d" % e, align_bytes=64)
+            for e in range(LAYERS * DIRECTIONS)
         ]
         w_planes = [keep.tile([P, GATE_BLOCKS * HIDDEN], U8, name="w_planes%d" % l, align_bytes=64) for l in range(LAYERS)]
         h_words = keep.tile([P, HALVES, CHUNK], U32, align_bytes=64)
@@ -86,11 +86,11 @@ def tile_lstmnetwork_pb_e_kernel(tc, h_layer0, w_ih_words, w_ih_scales, b_ih, b_
         bias_rows_f32 = keep.tile([P, P], F32)
         bias_ih = keep.tile([P, P // 2], F32)
         bias = keep.tile([P, P // 2], F32)
+        dummy = keep.tile([P, HIDDEN], BF16)
         warm_in = keep.tile([P, 1], F32)
         warm_out = keep.tile([P, 1], F32)
 
-        nc.scalar.dma_start(out=bias_rows[0 : P // 2, :], in_=b_ih.rearrange("l d (r c) -> (l d r) c", c=P))
-        nc.scalar.dma_start(out=bias_rows[P // 2 : P, :], in_=b_hh.rearrange("l d (r c) -> (l d r) c", c=P))
+        nc.vector.memset(dummy[:], 0.0)
         nc.vector.memset(warm_in[:], 0.0)
         nc.vector.memset(w_planes[1][:].bitcast(I32), 0)
         nc.scalar.activation(out=warm_out[:], in_=warm_in[:], func=SIGMOID)
@@ -110,35 +110,37 @@ def tile_lstmnetwork_pb_e_kernel(tc, h_layer0, w_ih_words, w_ih_scales, b_ih, b_
                     in_=groups[:, 4 * quadrant : 4 * quadrant + 4, :].bitcast(I32),
                 )
 
-        def word_bytes(e, first, columns):
+        def load_words(e, first, columns):
             some = slice(first * PACK, (first + columns) * PACK)
-            return w_words[e][:, some], w_ih_words[e].rearrange("p n t -> p (n t)")[:, some]
+            in_hbm = w_ih_words[e * PASSES : (e + 1) * PASSES].rearrange("g p n t -> p g (n t)")
+            nc.sync.dma_start(out=w_words[e][:, :, some].bitcast(I32), in_=in_hbm[:, :, some].bitcast(I32))
 
-        def load_first_layer_words(d):
-            for pair in range(PAIRS):
-                for block in (BLOCK_I, BLOCK_G, BLOCK_O):
-                    for k_pass in range(PASSES):
-                        in_sbuf, in_hbm = word_bytes(d * PASSES + k_pass, block * HIDDEN + pair * PAIR * P, PAIR * P)
-                        nc.sync.dma_start(out=in_sbuf.bitcast(I32), in_=in_hbm.bitcast(I32))
+        def load_pair_words(d, pair, blocks=(BLOCK_I, BLOCK_G, BLOCK_O)):
+            for block in blocks:
+                load_words(d, block * HIDDEN + pair * PAIR * P, PAIR * P)
 
         def load_second_layer_words(d):
-            for first_block, blocks in ((BLOCK_I, 1), (BLOCK_G, 2)):
-                for k_pass in range(PASSES):
-                    e = GROUPS_PER_LAYER + d * PASSES + k_pass
-                    in_sbuf, in_hbm = word_bytes(e, first_block * HIDDEN, blocks * HIDDEN)
-                    nc.sync.dma_start(out=in_sbuf.bitcast(I32), in_=in_hbm.bitcast(I32))
+            load_words(DIRECTIONS + d, BLOCK_I * HIDDEN, HIDDEN)
+            load_words(DIRECTIONS + d, BLOCK_G * HIDDEN, 2 * HIDDEN)
 
-        load_planes(0)
         load_tokens(0)
-        load_first_layer_words(0)
+        load_pair_words(0, 0, (BLOCK_I,))
+        load_planes(0)
+        nc.sync.dma_start(out=bias_rows[0 : P // 2, :], in_=b_ih.rearrange("l d (r c) -> (l d r) c", c=P))
+        nc.sync.dma_start(out=bias_rows[P // 2 : P, :], in_=b_hh.rearrange("l d (r c) -> (l d r) c", c=P))
+        load_pair_words(0, 0, (BLOCK_G, BLOCK_O))
         load_tokens(1)
-        load_first_layer_words(1)
+        load_pair_words(0, 1)
+        load_pair_words(1, 0)
+        load_pair_words(1, 1)
         load_planes(1)
         load_second_layer_words(0)
 
         grouped_of = {}
 
-        def group_input(half):
+        input_of = {}
+
+        def turn_input(half):
             layer, c, k_pass = half_place(half)
             turned = turn_banks.tile([P, 2, CHUNK], F32, tag="turned")
             for i in range(TOKEN_TILES):
@@ -149,6 +151,11 @@ def tile_lstmnetwork_pb_e_kernel(tc, h_layer0, w_ih_words, w_ih_scales, b_ih, b_
                         pairs[:, k_pass * (K_PASS // 2) + u : (k_pass + 1) * (K_PASS // 2) : 2],
                         identity[:],
                     )
+            input_of[half] = turned
+
+        def group_input(half):
+            layer, c, k_pass = half_place(half)
+            turned = input_of[half]
             grouped = stage.tile([P, CHUNK, PACK], BF16, tag="grouped", align_bytes=64)
             if c == 0:
                 nc.scalar.copy(out=grouped[:].bitcast(F32), in_=turned[:].rearrange("p u n -> p n u"))
@@ -161,6 +168,11 @@ def tile_lstmnetwork_pb_e_kernel(tc, h_layer0, w_ih_words, w_ih_scales, b_ih, b_
             grouped = stage.tile([P, CHUNK, PACK], BF16, tag="grouped", align_bytes=64)
             nc.vector.tensor_copy(out=grouped[:], in_=fetched_of[half][:].rearrange("p t n -> p n t"))
             grouped_of[half] = grouped
+
+        def keep_warm(count):
+            unread = gate_banks.tile([P, HIDDEN], F32, name="unread", tag="oo")
+            for n in range(count):
+                nc.tensor.matmul(unread[:], lhsT=dummy[:, 0:P], rhs=dummy[:], start=True, stop=True)
 
         def quantise(half):
             nc.vector.quantize_mx(
@@ -190,7 +202,7 @@ def tile_lstmnetwork_pb_e_kernel(tc, h_layer0, w_ih_words, w_ih_scales, b_ih, b_
                 half = (layer * CHUNKS + c) * PASSES + k_pass
                 nc.tensor.matmul_mx(
                     out=acc,
-                    lhsT=w_words[layer * DIRECTIONS * PASSES + in_layer][:, first * PACK : (first + P) * PACK].bitcast(FP8X4),
+                    lhsT=w_words[layer * DIRECTIONS + d][:, k_pass, first * PACK : (first + P) * PACK].bitcast(FP8X4),
                     lhsT_scale=w_planes[layer][4 * in_layer : P, first : first + P],
                     rhs=h_words[:, half, :].bitcast(FP8X4),
                     rhs_scale=h_planes[:, half, :],
@@ -258,10 +270,15 @@ def tile_lstmnetwork_pb_e_kernel(tc, h_layer0, w_ih_words, w_ih_scales, b_ih, b_
                 in_=result[:],
             )
 
-        for half in range(PASSES):
-            group_input(half)
+        keep_warm(5)
+        turn_input(0)
+        group_input(0)
+        keep_warm(1)
+        turn_input(1)
+        group_input(1)
         for half in range(PASSES):
             quantise(half)
+        keep_warm(3)
         spread_biases()
         for unit in range(AHEAD):
             multiply(unit)
@@ -301,5 +318,8 @@ def tile_lstmnetwork_pb_e_kernel(tc, h_layer0, w_ih_words, w_ih_scales, b_ih, b_
                 turn(step, 0, 1)
             if step < UNITS_PER_LAYER:
                 hand_over(step, 0)
+            if step == 0:
+                for k_pass in range(PASSES):
+                    turn_input(PASSES + k_pass)
             if step + AHEAD < UNITS:
                 multiply(step + AHEAD)

@@ -27,16 +27,13 @@ GROUPS_PER_LAYER = DIRECTIONS * PASSES
 GATE_BLOCKS = 4
 BLOCK_I, BLOCK_G, BLOCK_O = 0, 2, 3
 TILES_PER_BLOCK = HIDDEN // P
-CHUNK = 256
-CHUNKS = TOKENS // CHUNK
-TOKEN_TILES = CHUNK // P
+NARROW = 256
+CHUNKS = TOKENS // NARROW
+TOKEN_TILES = NARROW // P
 PAIR = 2
 PAIRS = TILES_PER_BLOCK // PAIR
-UNITS_PER_CHUNK = DIRECTIONS * PAIRS
-UNITS_PER_LAYER = CHUNKS * UNITS_PER_CHUNK
-UNITS = LAYERS * UNITS_PER_LAYER
+COLUMNS = 512
 AHEAD = 2
-HALVES = LAYERS * CHUNKS * PASSES
 
 FLOPS = 2 * TOKENS * FEATURES * 3 * HIDDEN * LAYERS * DIRECTIONS
 BYTES = (
@@ -48,17 +45,19 @@ BYTES = (
 )
 
 
-def unit_place(unit):
-    layer, rest = divmod(unit, UNITS_PER_LAYER)
-    chunk, rest = divmod(rest, UNITS_PER_CHUNK)
-    direction, pair = divmod(rest, PAIRS)
-    return layer, chunk, direction, pair
+def list_units():
+    units = []
+    for layer in range(LAYERS):
+        for token in (0, NARROW):
+            if token:
+                units += [(layer, 1, tile, 1, 0, TOKENS) for tile in range(PAIR, TILES_PER_BLOCK)]
+            units += [(layer, d, pair * PAIR, PAIR, token, NARROW) for d, pair in (((1, 0), (0, 0), (0, 1)) if token else ((0, 0), (0, 1), (1, 0)))]
+    return units
 
 
-def half_place(half):
-    layer, rest = divmod(half, CHUNKS * PASSES)
-    chunk, k_pass = divmod(rest, PASSES)
-    return layer, chunk, k_pass
+UNIT_LIST = list_units()
+UNITS = len(UNIT_LIST)
+UNITS_PER_LAYER = UNITS // LAYERS
 
 
 def tile_lstmnetwork_pb_e_kernel(tc, h_layer0, w_ih_words, w_ih_scales, b_ih, b_hh, out):
@@ -69,7 +68,7 @@ def tile_lstmnetwork_pb_e_kernel(tc, h_layer0, w_ih_words, w_ih_scales, b_ih, b_
         keep = ctx.enter_context(tc.tile_pool(name="keep", bufs=1))
         stage = ctx.enter_context(tc.tile_pool(name="stage", bufs=2))
         work = ctx.enter_context(tc.tile_pool(name="work", bufs=2))
-        leave = ctx.enter_context(tc.tile_pool(name="leave", bufs=3))
+        leave = ctx.enter_context(tc.tile_pool(name="leave", bufs=4))
         gate_banks = ctx.enter_context(tc.psum_pool(name="gate_banks", bufs=AHEAD))
         turn_banks = ctx.enter_context(tc.psum_pool(name="turn_banks", bufs=2))
 
@@ -79,8 +78,11 @@ def tile_lstmnetwork_pb_e_kernel(tc, h_layer0, w_ih_words, w_ih_scales, b_ih, b_
             for e in range(LAYERS * DIRECTIONS)
         ]
         w_planes = [keep.tile([P, GATE_BLOCKS * HIDDEN], U8, name="w_planes%d" % l, align_bytes=64) for l in range(LAYERS)]
-        h_words = keep.tile([P, HALVES, CHUNK], U32, align_bytes=64)
-        h_planes = keep.tile([P, HALVES, CHUNK], U8, align_bytes=64)
+        h_words = keep.tile([P, LAYERS * PASSES, TOKENS], U32, align_bytes=64)
+        h_planes = keep.tile([P, LAYERS * PASSES, TOKENS], U8, align_bytes=64)
+        fetched = [
+            [keep.tile([P, PACK, NARROW], BF16, name="fetched%d%d" % (d, c)) for c in range(CHUNKS)] for d in range(DIRECTIONS)
+        ]
         identity = keep.tile([P, P], F32)
         bias_rows = keep.tile([P, P], BF16)
         bias_rows_f32 = keep.tile([P, P], F32)
@@ -97,7 +99,7 @@ def tile_lstmnetwork_pb_e_kernel(tc, h_layer0, w_ih_words, w_ih_scales, b_ih, b_
         make_identity(nc, identity[:])
 
         def load_tokens(c):
-            rows = h_layer0[c * CHUNK : (c + 1) * CHUNK, :].rearrange("(i p) f -> p i f", p=P)
+            rows = h_layer0[c * NARROW : (c + 1) * NARROW, :].rearrange("(i p) f -> p i f", p=P)
             for k_pass in range(PASSES):
                 some = slice(k_pass * K_PASS, (k_pass + 1) * K_PASS)
                 nc.sync.dma_start(out=x_rows[c][:, :, some], in_=rows[:, :, some])
@@ -115,7 +117,7 @@ def tile_lstmnetwork_pb_e_kernel(tc, h_layer0, w_ih_words, w_ih_scales, b_ih, b_
             in_hbm = w_ih_words[e * PASSES : (e + 1) * PASSES].rearrange("g p n t -> p g (n t)")
             nc.sync.dma_start(out=w_words[e][:, :, some].bitcast(I32), in_=in_hbm[:, :, some].bitcast(I32))
 
-        def load_pair_words(d, pair, blocks=(BLOCK_I, BLOCK_G, BLOCK_O)):
+        def load_first_layer_words(d, pair, blocks):
             for block in blocks:
                 load_words(d, block * HIDDEN + pair * PAIR * P, PAIR * P)
 
@@ -124,25 +126,24 @@ def tile_lstmnetwork_pb_e_kernel(tc, h_layer0, w_ih_words, w_ih_scales, b_ih, b_
             load_words(DIRECTIONS + d, BLOCK_G * HIDDEN, 2 * HIDDEN)
 
         load_tokens(0)
-        load_pair_words(0, 0, (BLOCK_I,))
+        load_first_layer_words(0, 0, (BLOCK_I,))
         load_planes(0)
         nc.sync.dma_start(out=bias_rows[0 : P // 2, :], in_=b_ih.rearrange("l d (r c) -> (l d r) c", c=P))
         nc.sync.dma_start(out=bias_rows[P // 2 : P, :], in_=b_hh.rearrange("l d (r c) -> (l d r) c", c=P))
-        load_pair_words(0, 0, (BLOCK_G, BLOCK_O))
+        load_first_layer_words(0, 0, (BLOCK_G, BLOCK_O))
+        load_first_layer_words(0, 1, (BLOCK_I, BLOCK_G, BLOCK_O))
         load_tokens(1)
-        load_pair_words(0, 1)
-        load_pair_words(1, 0)
-        load_pair_words(1, 1)
+        for pair in range(PAIRS):
+            load_first_layer_words(1, pair, (BLOCK_I, BLOCK_G, BLOCK_O))
         load_planes(1)
         load_second_layer_words(0)
 
         grouped_of = {}
 
-        input_of = {}
+        turned_input = {}
 
-        def turn_input(half):
-            layer, c, k_pass = half_place(half)
-            turned = turn_banks.tile([P, 2, CHUNK], F32, tag="turned")
+        def turn_input(c, k_pass):
+            turned = turn_banks.tile([P, 2, NARROW], F32, tag="turned")
             for i in range(TOKEN_TILES):
                 pairs = x_rows[c][:, i, :].bitcast(F32)
                 for u in range(2):
@@ -151,34 +152,28 @@ def tile_lstmnetwork_pb_e_kernel(tc, h_layer0, w_ih_words, w_ih_scales, b_ih, b_
                         pairs[:, k_pass * (K_PASS // 2) + u : (k_pass + 1) * (K_PASS // 2) : 2],
                         identity[:],
                     )
-            input_of[half] = turned
+            turned_input[k_pass, c] = turned
 
-        def group_input(half):
-            layer, c, k_pass = half_place(half)
-            turned = input_of[half]
-            grouped = stage.tile([P, CHUNK, PACK], BF16, tag="grouped", align_bytes=64)
+        def group_input(c, k_pass):
+            turned = turned_input[k_pass, c]
+            grouped = stage.tile([P, NARROW, PACK], BF16, tag="grouped", align_bytes=64)
             if c == 0:
                 nc.scalar.copy(out=grouped[:].bitcast(F32), in_=turned[:].rearrange("p u n -> p n u"))
             else:
                 nc.vector.tensor_copy(out=grouped[:].bitcast(F32), in_=turned[:].rearrange("p u n -> p n u"))
-            grouped_of[half] = grouped
+            grouped_of[0, k_pass, c] = grouped
 
-        def group_parked(half):
-            layer, c, k_pass = half_place(half)
-            grouped = stage.tile([P, CHUNK, PACK], BF16, tag="grouped", align_bytes=64)
-            nc.vector.tensor_copy(out=grouped[:], in_=fetched_of[half][:].rearrange("p t n -> p n t"))
-            grouped_of[half] = grouped
+        def group_hidden(c, d):
+            grouped = stage.tile([P, NARROW, PACK], BF16, tag="grouped", align_bytes=64)
+            nc.vector.tensor_copy(out=grouped[:], in_=fetched[d][c][:].rearrange("p t n -> p n t"))
+            grouped_of[1, d, c] = grouped
 
-        def keep_warm(count):
-            unread = gate_banks.tile([P, HIDDEN], F32, name="unread", tag="oo")
-            for n in range(count):
-                nc.tensor.matmul(unread[:], lhsT=dummy[:, 0:P], rhs=dummy[:], start=True, stop=True)
-
-        def quantise(half):
+        def quantise(layer, k_pass, c):
+            some = slice(c * NARROW, (c + 1) * NARROW)
             nc.vector.quantize_mx(
-                out=h_words[:, half, :].bitcast(FP8X4),
-                scales=h_planes[:, half, :],
-                in_=grouped_of[half][:].rearrange("p n t -> p (n t)"),
+                out=h_words[:, layer * PASSES + k_pass, some].bitcast(FP8X4),
+                scales=h_planes[:, layer * PASSES + k_pass, some],
+                in_=grouped_of[layer, k_pass, c][:].rearrange("p n t -> p (n t)"),
             )
 
         def spread_biases():
@@ -188,138 +183,206 @@ def tile_lstmnetwork_pb_e_kernel(tc, h_layer0, w_ih_words, w_ih_scales, b_ih, b_
             nc.vector.tensor_copy(out=bias_ih[:], in_=bias_turned[:, 0 : P // 2])
             nc.vector.tensor_tensor(out=bias[:], in0=bias_ih[:], in1=bias_turned[:, P // 2 : P], op=ADD)
 
+        def keep_warm(count):
+            unread = gate_banks.tile([P, HIDDEN], F32, name="unread", tag="bank2")
+            for n in range(count):
+                nc.tensor.matmul(unread[:], lhsT=dummy[:, 0:P], rhs=dummy[:], start=True, stop=True)
+
         banks_of = {}
-        cell_of = {}
+        acts_of = {}
         h_of = {}
         turned_of = {}
-        fetched_of = {}
+        result_of = {}
 
-        def gate_group(acc, unit, block, j):
-            layer, c, d, pair = unit_place(unit)
-            first = block * HIDDEN + (pair * PAIR + j) * P
-            for k_pass in range(PASSES):
-                in_layer = d * PASSES + k_pass
-                half = (layer * CHUNKS + c) * PASSES + k_pass
-                nc.tensor.matmul_mx(
-                    out=acc,
-                    lhsT=w_words[layer * DIRECTIONS + d][:, k_pass, first * PACK : (first + P) * PACK].bitcast(FP8X4),
-                    lhsT_scale=w_planes[layer][4 * in_layer : P, first : first + P],
-                    rhs=h_words[:, half, :].bitcast(FP8X4),
-                    rhs_scale=h_planes[:, half, :],
-                    start=(k_pass == 0),
-                    stop=(k_pass == PASSES - 1),
-                )
+        def is_wide(unit):
+            return 0 <= unit < UNITS and UNIT_LIST[unit][3] == 1
 
         def multiply(unit):
-            ig = [gate_banks.tile([P, 2, CHUNK], F32, name="ig%d" % j, tag="ig%d" % j) for j in range(PAIR)]
-            oo = gate_banks.tile([P, PAIR, CHUNK], F32, tag="oo")
-            for j in range(PAIR):
-                gate_group(ig[j][:, 0, :], unit, BLOCK_I, j)
-                gate_group(ig[j][:, 1, :], unit, BLOCK_G, j)
-            for j in range(PAIR):
-                gate_group(oo[:, j, :], unit, BLOCK_O, j)
-            banks_of[unit] = (ig, oo)
+            layer, d, first_tile, tiles, first_token, tokens = UNIT_LIST[unit]
+            banks = [gate_banks.tile([P, tiles, tokens], F32, name="bank%d" % b, tag="bank%d" % b) for b in range(3)]
+            order = [(0, j) for j in range(tiles)] + [(1, j) for j in range(tiles)] + [(2, j) for j in range(tiles)]
+            for b, j in order:
+                first = (BLOCK_I, BLOCK_G, BLOCK_O)[b] * HIDDEN + (first_tile + j) * P
+                for k_pass in range(PASSES):
+                    in_layer = d * PASSES + k_pass
+                    some = slice(first_token, first_token + tokens)
+                    nc.tensor.matmul_mx(
+                        out=banks[b][:, j, :],
+                        lhsT=w_words[layer * DIRECTIONS + d][:, k_pass, first * PACK : (first + P) * PACK].bitcast(FP8X4),
+                        lhsT_scale=w_planes[layer][4 * in_layer : P, first : first + P],
+                        rhs=h_words[:, layer * PASSES + k_pass, some].bitcast(FP8X4),
+                        rhs_scale=h_planes[:, layer * PASSES + k_pass, some],
+                        start=(k_pass == 0),
+                        stop=(k_pass == PASSES - 1),
+                    )
+            banks_of[unit] = banks
 
-        def bias_column(unit, block, j):
-            layer, c, d, pair = unit_place(unit)
-            r = ((layer * DIRECTIONS + d) * GATE_BLOCKS + block) * TILES_PER_BLOCK + pair * PAIR + j
-            return bias[:, r : r + 1]
-
-        def cell_state(unit, j):
-            ig, oo = banks_of[unit]
-            ig_act = work.tile([P, 2, CHUNK], F32, tag="ig_act%d" % j)
-            cell = work.tile([P, CHUNK], F32, tag="cell%d" % j)
-            nc.scalar.activation(out=ig_act[:, 0, :], in_=ig[j][:, 0, :], func=SIGMOID, bias=bias_column(unit, BLOCK_I, j))
-            nc.scalar.activation(out=ig_act[:, 1, :], in_=ig[j][:, 1, :], func=TANH, bias=bias_column(unit, BLOCK_G, j))
-            nc.vector.tensor_tensor(out=cell[:], in0=ig_act[:, 0, :], in1=ig_act[:, 1, :], op=MULT)
-            cell_of[unit, j] = cell
-
-        def hidden(unit, j):
-            ig, oo = banks_of[unit]
-            if j == 0 and unit < UNITS_PER_LAYER:
-                h_of[unit] = keep.tile([P, PAIR, CHUNK], BF16, name="h_first%d" % unit)
-            if j == 0 and unit >= UNITS_PER_LAYER:
-                h_of[unit] = leave.tile([P, PAIR, CHUNK], F32, name="h_last", tag="h_last")
-            oc_act = work.tile([P, 2, CHUNK], F32, tag="oc_act%d" % j)
-            nc.scalar.activation(out=oc_act[:, 0, :], in_=oo[:, j, :], func=SIGMOID, bias=bias_column(unit, BLOCK_O, j))
-            nc.scalar.activation(out=oc_act[:, 1, :], in_=cell_of[unit, j][:], func=TANH)
-            nc.vector.tensor_tensor(out=h_of[unit][:, j, :], in0=oc_act[:, 0, :], in1=oc_act[:, 1, :], op=MULT)
-
-        def hand_over(unit, j):
-            layer, c, d, pair = unit_place(unit)
-            half = (CHUNKS + c) * PASSES + d
-            if pair == 0 and j == 0:
-                fetched_of[half] = stage.tile([P, PACK, CHUNK], BF16, name="fetched", tag="fetched", bufs=3)
-            first = (pair * PAIR + j) * (P // PACK)
-            nc.sync.dma_start(out=fetched_of[half][first : first + P // PACK, :, :], in_=h_of[unit][:, j, :])
-
-        def turn(unit, first_tile=0, tiles=PAIR):
-            h_rows = turn_banks.tile([P, TOKEN_TILES, tiles, P], F32, tag="turned")
-            for j in range(tiles):
-                for i in range(TOKEN_TILES):
-                    nc.tensor.transpose(h_rows[:, i, j, :], h_of[unit][:, first_tile + j, i * P : (i + 1) * P], identity[:])
-            turned_of[unit] = h_rows
-
-        def store_rows(unit, first_tile=0, tiles=PAIR):
-            layer, c, d, pair = unit_place(unit)
-            first = d * HIDDEN + (pair * PAIR + first_tile) * P
-            result = leave.tile([P, TOKEN_TILES, tiles * P], F32, tag="result")
-            nc.vector.tensor_copy(out=result[:], in_=turned_of[unit][:].rearrange("p i j f -> p i (j f)"))
-            nc.sync.dma_start(
-                out=out_rows[c * CHUNK : (c + 1) * CHUNK, first : first + tiles * P].rearrange("(i p) f -> p i f", p=P),
-                in_=result[:],
+        def gate(unit, b, j):
+            layer, d, first_tile, tiles, first_token, tokens = UNIT_LIST[unit]
+            r = ((layer * DIRECTIONS + d) * GATE_BLOCKS + (BLOCK_I, BLOCK_G, BLOCK_O)[b]) * TILES_PER_BLOCK + first_tile + j
+            nc.scalar.activation(
+                out=acts_of[unit][b][:, j * tokens : (j + 1) * tokens],
+                in_=banks_of[unit][b][:, j, :],
+                func=(SIGMOID, TANH, SIGMOID)[b],
+                bias=bias[:, r : r + 1],
             )
 
+        def start_unit(unit):
+            acts_of[unit] = [work.tile([P, COLUMNS], F32, name="work%d" % k, tag="work%d" % k) for k in range(5)]
+            if unit < UNITS_PER_LAYER:
+                h_of[unit] = keep.tile([P, COLUMNS], BF16, name="h_first%d" % unit)
+            else:
+                h_of[unit] = leave.tile([P, COLUMNS], F32, name="h_last", tag="h_last")
+
+        def cell_state(unit, j):
+            i_act, g_act, o_act, cell, cell_tanh = acts_of[unit]
+            tokens = UNIT_LIST[unit][5]
+            some = slice(j * tokens, (j + 1) * tokens)
+            nc.vector.tensor_tensor(out=cell[:, some], in0=i_act[:, some], in1=g_act[:, some], op=MULT)
+
+        def squash(unit, some):
+            i_act, g_act, o_act, cell, cell_tanh = acts_of[unit]
+            nc.scalar.activation(out=cell_tanh[:, some], in_=cell[:, some], func=TANH)
+
+        def hidden(unit, some):
+            i_act, g_act, o_act, cell, cell_tanh = acts_of[unit]
+            nc.vector.tensor_tensor(out=h_of[unit][:, some], in0=o_act[:, some], in1=cell_tanh[:, some], op=MULT)
+
+        ALL = slice(0, COLUMNS)
+        PIECES = [slice(0, NARROW), slice(NARROW, COLUMNS)]
+
+        def hand_over(unit, piece):
+            layer, d, first_tile, tiles, first_token, tokens = UNIT_LIST[unit]
+            for k in range(COLUMNS // NARROW):
+                if piece.start <= k * NARROW < piece.stop:
+                    tile, c = (first_tile, k) if tiles == 1 else (first_tile + k, first_token // NARROW)
+                    rows = slice(tile * (P // PACK), (tile + 1) * (P // PACK))
+                    nc.sync.dma_start(out=fetched[d][c][rows, :, :], in_=h_of[unit][:, k * NARROW : (k + 1) * NARROW])
+
+        def turn(unit, tiles_now):
+            layer, d, first_tile, tiles, first_token, tokens = UNIT_LIST[unit]
+            h_rows = turn_banks.tile([P, tokens // P, len(tiles_now), P], F32, name="h_rows", tag="turned")
+            for k, j in enumerate(tiles_now):
+                for i in range(tokens // P):
+                    first = j * tokens + i * P
+                    nc.tensor.transpose(h_rows[:, i, k, :], h_of[unit][:, first : first + P], identity[:])
+            turned_of[unit] = h_rows
+
+        def store_rows(unit, tiles_now):
+            layer, d, first_tile, tiles, first_token, tokens = UNIT_LIST[unit]
+            width = PAIR * P if tiles == 1 or len(tiles_now) == PAIR else P
+            k = first_tile % PAIR if tiles == 1 else 0
+            if k == 0:
+                result_of[d] = leave.tile([P, tokens // P, width], F32, name="result", tag="result")
+            result = result_of[d]
+            taken = len(tiles_now) * P
+            nc.vector.tensor_copy(
+                out=result[:, :, k * P : k * P + taken], in_=turned_of[unit][:].rearrange("p i j f -> p i (j f)")
+            )
+            if k * P + taken == width:
+                first = d * HIDDEN + (first_tile - k + tiles_now[0]) * P
+                nc.sync.dma_start(
+                    out=out_rows[first_token : first_token + tokens, first : first + width].rearrange("(i p) f -> p i f", p=P),
+                    in_=result[:],
+                )
+
+        early_work = {
+            0: [(turn_input, (1, 0)), (turn_input, (1, 1))],
+            2: [(quantise, (0, 0, 1)), (quantise, (0, 1, 1))],
+            7: [(group_hidden, (0, 1))],
+            10: [(group_hidden, (1, 0))],
+        }
+        middle_work = {7: [(quantise, (1, 1, 0))], 10: [(quantise, (1, 0, 1))]}
+        late_work = {
+            1: [(group_input, (1, 0)), (group_input, (1, 1))],
+            5: [(group_hidden, (0, 0))],
+            6: [(quantise, (1, 0, 0))],
+            8: [(group_hidden, (1, 1))],
+            9: [(quantise, (1, 1, 1))],
+        }
+        first_step_for = {3: 2, 8: 7, 9: 7, 11: 10, 12: 10}
+        late_hidden = (6, 9)
+
+        def run_work(table, step):
+            for work_item, arguments in table.get(step, []):
+                work_item(*arguments)
+
         keep_warm(5)
-        turn_input(0)
-        group_input(0)
+        turn_input(0, 0)
+        group_input(0, 0)
         keep_warm(1)
-        turn_input(1)
-        group_input(1)
-        for half in range(PASSES):
-            quantise(half)
+        turn_input(0, 1)
+        group_input(0, 1)
+        for k_pass in range(PASSES):
+            quantise(0, k_pass, 0)
         keep_warm(3)
         spread_biases()
-        for unit in range(AHEAD):
-            multiply(unit)
-        for step in range(UNITS + 1):
-            phase, k_pass = divmod(step + AHEAD + 1, UNITS_PER_CHUNK)
-            half = phase * PASSES + k_pass
-            makes_operand = k_pass < PASSES and half < HALVES
-            if step < UNITS:
-                cell_state(step, 0)
-            if UNITS_PER_LAYER <= step - 2 < UNITS - 2:
-                store_rows(step - 2)
-            if 0 <= step - 1 < UNITS:
-                hidden(step - 1, 1)
-            if 0 <= step - 1 < UNITS_PER_LAYER:
-                hand_over(step - 1, 1)
-            if step == UNITS_PER_CHUNK:
+        multiply(0)
+        multiply(1)
+        next_unit = 2
+        to_hide, to_turn, to_store = [], [], []
+
+        def finish(unit, pieces):
+            for piece in pieces:
+                hidden(unit, piece)
+                if unit < UNITS_PER_LAYER:
+                    hand_over(unit, piece)
+            if unit >= UNITS_PER_LAYER:
+                to_turn.append(unit)
+
+        for step in range(UNITS):
+            tiles = UNIT_LIST[step][3]
+            start_unit(step)
+            if step == 6:
                 load_second_layer_words(1)
-            if UNITS_PER_LAYER <= step - 1 < UNITS - 1:
-                turn(step - 1)
-            if step == UNITS:
-                store_rows(UNITS - 1, 0, 1)
-                turn(UNITS - 1, 1, 1)
-                store_rows(UNITS - 1, 1, 1)
-            if step < UNITS:
-                cell_state(step, 1)
-            if step == UNITS - 1:
-                store_rows(step - 1)
-            if makes_operand and half < CHUNKS * PASSES:
-                group_input(half)
-            if makes_operand and half >= CHUNKS * PASSES:
-                group_parked(half)
-            if makes_operand:
-                quantise(half)
-            if step < UNITS:
-                hidden(step, 0)
-            if step == UNITS - 1:
-                turn(step, 0, 1)
-            if step < UNITS_PER_LAYER:
-                hand_over(step, 0)
-            if step == 0:
-                for k_pass in range(PASSES):
-                    turn_input(PASSES + k_pass)
-            if step + AHEAD < UNITS:
-                multiply(step + AHEAD)
+            storing = list(to_store)
+            to_store.clear()
+            for unit in to_turn:
+                turn(unit, range(UNIT_LIST[unit][3]))
+                to_store.append(unit)
+            to_turn.clear()
+            run_work(early_work, step)
+            for j in range(tiles):
+                gate(step, 0, j)
+            for j in range(tiles):
+                gate(step, 1, j)
+                cell_state(step, j)
+                if j == 0:
+                    run_work(middle_work, step)
+            if is_wide(step) and is_wide(step - 1):
+                squash(step - 1, ALL)
+                to_hide.append(step - 1)
+            for unit in storing:
+                store_rows(unit, range(UNIT_LIST[unit][3]))
+            for unit in to_hide:
+                finish(unit, [ALL])
+            to_hide.clear()
+            run_work(late_work, step)
+            final = step == UNITS - 1
+            for j in range(tiles):
+                gate(step, 2, j)
+                if final:
+                    squash(step, PIECES[j])
+                    hidden(step, PIECES[j])
+                    for unit in to_store:
+                        store_rows(unit, range(PAIR))
+                    to_store.clear()
+                    if j == 1:
+                        store_rows(step, [0])
+                    turn(step, [j])
+            if final:
+                store_rows(step, [1])
+            if tiles == PAIR and not final:
+                squash(step, ALL)
+                if step in late_hidden:
+                    to_hide.append(step)
+                else:
+                    finish(step, [ALL])
+            if is_wide(step) and not is_wide(step + 1):
+                squash(step, ALL)
+                finish(step, PIECES if step < UNITS_PER_LAYER else [ALL])
+            while next_unit < UNITS and first_step_for.get(next_unit, next_unit - AHEAD) <= step:
+                multiply(next_unit)
+                next_unit += 1
+                if next_unit == UNITS_PER_LAYER:
+                    keep_warm(8)

@@ -67,8 +67,8 @@ def tile_lstmnetwork_pb_e_kernel(tc, h_layer0, w_ih_words, w_ih_scales, b_ih, b_
         ctx.enter_context(tc.manual_schedule())
         keep = ctx.enter_context(tc.tile_pool(name="keep", bufs=1))
         stage = ctx.enter_context(tc.tile_pool(name="stage", bufs=2))
-        work = ctx.enter_context(tc.tile_pool(name="work", bufs=2))
-        leave = ctx.enter_context(tc.tile_pool(name="leave", bufs=4))
+        work = ctx.enter_context(tc.tile_pool(name="work", bufs=3))
+        leave = ctx.enter_context(tc.tile_pool(name="leave", bufs=5))
         gate_banks = ctx.enter_context(tc.psum_pool(name="gate_banks", bufs=AHEAD))
         turn_banks = ctx.enter_context(tc.psum_pool(name="turn_banks", bufs=2))
 
@@ -97,6 +97,9 @@ def tile_lstmnetwork_pb_e_kernel(tc, h_layer0, w_ih_words, w_ih_scales, b_ih, b_
         nc.vector.memset(w_planes[1][:].bitcast(I32), 0)
         nc.scalar.activation(out=warm_out[:], in_=warm_in[:], func=SIGMOID)
         make_identity(nc, identity[:])
+
+        nc.gpsimd.dma_start(out=bias_rows[0 : P // 2, :], in_=b_ih.rearrange("l d (r c) -> (l d r) c", c=P))
+        nc.gpsimd.dma_start(out=bias_rows[P // 2 : P, :], in_=b_hh.rearrange("l d (r c) -> (l d r) c", c=P))
 
         def load_tokens(c):
             rows = h_layer0[c * NARROW : (c + 1) * NARROW, :].rearrange("(i p) f -> p i f", p=P)
@@ -128,8 +131,6 @@ def tile_lstmnetwork_pb_e_kernel(tc, h_layer0, w_ih_words, w_ih_scales, b_ih, b_
         load_tokens(0)
         load_first_layer_words(0, 0, (BLOCK_I,))
         load_planes(0)
-        nc.sync.dma_start(out=bias_rows[0 : P // 2, :], in_=b_ih.rearrange("l d (r c) -> (l d r) c", c=P))
-        nc.sync.dma_start(out=bias_rows[P // 2 : P, :], in_=b_hh.rearrange("l d (r c) -> (l d r) c", c=P))
         load_first_layer_words(0, 0, (BLOCK_G, BLOCK_O))
         load_first_layer_words(0, 1, (BLOCK_I, BLOCK_G, BLOCK_O))
         load_tokens(1)
@@ -177,14 +178,13 @@ def tile_lstmnetwork_pb_e_kernel(tc, h_layer0, w_ih_words, w_ih_scales, b_ih, b_
             )
 
         def spread_biases():
-            nc.vector.tensor_copy(out=bias_rows_f32[:], in_=bias_rows[:])
             bias_turned = turn_banks.tile([P, P], F32, tag="turned")
             nc.tensor.transpose(bias_turned[:], bias_rows_f32[:], identity[:])
             nc.vector.tensor_copy(out=bias_ih[:], in_=bias_turned[:, 0 : P // 2])
             nc.vector.tensor_tensor(out=bias[:], in0=bias_ih[:], in1=bias_turned[:, P // 2 : P], op=ADD)
 
-        def keep_warm(count):
-            unread = gate_banks.tile([P, HIDDEN], F32, name="unread", tag="bank2")
+        def keep_warm(count, pool, tag):
+            unread = pool.tile([P, HIDDEN], F32, name="unread", tag=tag)
             for n in range(count):
                 nc.tensor.matmul(unread[:], lhsT=dummy[:, 0:P], rhs=dummy[:], start=True, stop=True)
 
@@ -301,26 +301,27 @@ def tile_lstmnetwork_pb_e_kernel(tc, h_layer0, w_ih_words, w_ih_scales, b_ih, b_
             9: [(quantise, (1, 1, 1))],
         }
         first_step_for = {3: 2, 8: 7, 9: 7, 11: 10, 12: 10}
-        late_hidden = (6, 9)
+        at_once = (4, 7)
 
         def run_work(table, step):
             for work_item, arguments in table.get(step, []):
                 work_item(*arguments)
 
-        keep_warm(5)
+        keep_warm(5, gate_banks, "bank2")
         turn_input(0, 0)
         group_input(0, 0)
-        keep_warm(1)
+        keep_warm(1, gate_banks, "bank2")
         turn_input(0, 1)
         group_input(0, 1)
+        nc.vector.tensor_copy(out=bias_rows_f32[:], in_=bias_rows[:])
         for k_pass in range(PASSES):
             quantise(0, k_pass, 0)
-        keep_warm(3)
+        keep_warm(3, gate_banks, "bank2")
         spread_biases()
         multiply(0)
         multiply(1)
         next_unit = 2
-        to_hide, to_turn, to_store = [], [], []
+        to_turn, to_store = [], []
 
         def finish(unit, pieces):
             for piece in pieces:
@@ -330,17 +331,19 @@ def tile_lstmnetwork_pb_e_kernel(tc, h_layer0, w_ih_words, w_ih_scales, b_ih, b_
             if unit >= UNITS_PER_LAYER:
                 to_turn.append(unit)
 
-        for step in range(UNITS):
-            tiles = UNIT_LIST[step][3]
-            start_unit(step)
-            if step == 6:
-                load_second_layer_words(1)
-            storing = list(to_store)
-            to_store.clear()
+        def turn_all():
             for unit in to_turn:
                 turn(unit, range(UNIT_LIST[unit][3]))
                 to_store.append(unit)
             to_turn.clear()
+
+        waiting = None
+        for step in range(UNITS):
+            tiles = UNIT_LIST[step][3]
+            final = step == UNITS - 1
+            start_unit(step)
+            if step == 6:
+                load_second_layer_words(1)
             run_work(early_work, step)
             for j in range(tiles):
                 gate(step, 0, j)
@@ -349,16 +352,18 @@ def tile_lstmnetwork_pb_e_kernel(tc, h_layer0, w_ih_words, w_ih_scales, b_ih, b_
                 cell_state(step, j)
                 if j == 0:
                     run_work(middle_work, step)
-            if is_wide(step) and is_wide(step - 1):
-                squash(step - 1, ALL)
-                to_hide.append(step - 1)
+            if waiting is not None:
+                squash(waiting, ALL)
+            storing = list(to_store)
+            to_store.clear()
+            if waiting is not None:
+                finish(waiting, [ALL])
+                waiting = None
+            if next_unit == UNITS:
+                turn_all()
             for unit in storing:
                 store_rows(unit, range(UNIT_LIST[unit][3]))
-            for unit in to_hide:
-                finish(unit, [ALL])
-            to_hide.clear()
             run_work(late_work, step)
-            final = step == UNITS - 1
             for j in range(tiles):
                 gate(step, 2, j)
                 if final:
@@ -372,17 +377,16 @@ def tile_lstmnetwork_pb_e_kernel(tc, h_layer0, w_ih_words, w_ih_scales, b_ih, b_
                     turn(step, [j])
             if final:
                 store_rows(step, [1])
-            if tiles == PAIR and not final:
+            elif step in at_once:
                 squash(step, ALL)
-                if step in late_hidden:
-                    to_hide.append(step)
-                else:
-                    finish(step, [ALL])
-            if is_wide(step) and not is_wide(step + 1):
-                squash(step, ALL)
-                finish(step, PIECES if step < UNITS_PER_LAYER else [ALL])
+                finish(step, PIECES)
+            else:
+                waiting = step
             while next_unit < UNITS and first_step_for.get(next_unit, next_unit - AHEAD) <= step:
                 multiply(next_unit)
                 next_unit += 1
                 if next_unit == UNITS_PER_LAYER:
-                    keep_warm(8)
+                    keep_warm(8, turn_banks, "turned")
+            turn_all()
+            if step == 8:
+                keep_warm(5, turn_banks, "turned")

@@ -85,7 +85,7 @@ def tile_lstmnetwork_pb_e_kernel(tc, h_layer0, w_ih_words, w_ih_scales, b_ih, b_
         ]
         identity = keep.tile([P, P], F32)
         bias_rows = keep.tile([P, P], BF16)
-        bias_rows_f32 = keep.tile([P, P], F32)
+        identity_bf16 = keep.tile([P, P], BF16)
         bias_ih = keep.tile([P, P // 2], F32)
         bias = keep.tile([P, P // 2], F32)
         dummy = keep.tile([P, HIDDEN], BF16)
@@ -97,9 +97,7 @@ def tile_lstmnetwork_pb_e_kernel(tc, h_layer0, w_ih_words, w_ih_scales, b_ih, b_
         nc.vector.memset(w_planes[1][:].bitcast(I32), 0)
         nc.scalar.activation(out=warm_out[:], in_=warm_in[:], func=SIGMOID)
         make_identity(nc, identity[:])
-
-        nc.gpsimd.dma_start(out=bias_rows[0 : P // 2, :], in_=b_ih.rearrange("l d (r c) -> (l d r) c", c=P))
-        nc.gpsimd.dma_start(out=bias_rows[P // 2 : P, :], in_=b_hh.rearrange("l d (r c) -> (l d r) c", c=P))
+        make_identity(nc, identity_bf16[:])
 
         def load_tokens(c):
             rows = h_layer0[c * NARROW : (c + 1) * NARROW, :].rearrange("(i p) f -> p i f", p=P)
@@ -131,6 +129,8 @@ def tile_lstmnetwork_pb_e_kernel(tc, h_layer0, w_ih_words, w_ih_scales, b_ih, b_
         load_tokens(0)
         load_first_layer_words(0, 0, (BLOCK_I,))
         load_planes(0)
+        nc.sync.dma_start(out=bias_rows[0 : P // 2, :], in_=b_ih.rearrange("l d (r c) -> (l d r) c", c=P))
+        nc.sync.dma_start(out=bias_rows[P // 2 : P, :], in_=b_hh.rearrange("l d (r c) -> (l d r) c", c=P))
         load_first_layer_words(0, 0, (BLOCK_G, BLOCK_O))
         load_first_layer_words(0, 1, (BLOCK_I, BLOCK_G, BLOCK_O))
         load_tokens(1)
@@ -178,8 +178,8 @@ def tile_lstmnetwork_pb_e_kernel(tc, h_layer0, w_ih_words, w_ih_scales, b_ih, b_
             )
 
         def spread_biases():
-            bias_turned = turn_banks.tile([P, P], F32, tag="turned")
-            nc.tensor.transpose(bias_turned[:], bias_rows_f32[:], identity[:])
+            bias_turned = turn_banks.tile([P, P], BF16, tag="turned")
+            nc.tensor.transpose(bias_turned[:], bias_rows[:], identity_bf16[:])
             nc.vector.tensor_copy(out=bias_ih[:], in_=bias_turned[:, 0 : P // 2])
             nc.vector.tensor_tensor(out=bias[:], in0=bias_ih[:], in1=bias_turned[:, P // 2 : P], op=ADD)
 
@@ -313,7 +313,6 @@ def tile_lstmnetwork_pb_e_kernel(tc, h_layer0, w_ih_words, w_ih_scales, b_ih, b_
         keep_warm(1, gate_banks, "bank2")
         turn_input(0, 1)
         group_input(0, 1)
-        nc.vector.tensor_copy(out=bias_rows_f32[:], in_=bias_rows[:])
         for k_pass in range(PASSES):
             quantise(0, k_pass, 0)
         keep_warm(3, gate_banks, "bank2")

@@ -92,8 +92,9 @@ def tile_lstmnetwork_pb_e_kernel(tc, h_layer0, w_ih_words, w_ih_scales, b_ih, b_
         warm_in = keep.tile([P, 1], F32)
         warm_out = keep.tile([P, 1], F32)
 
-        nc.vector.memset(dummy[:], 0.0)
         nc.vector.memset(warm_in[:], 0.0)
+        nc.vector.memset(w_planes[0][:].bitcast(I32), 0)
+        nc.vector.memset(dummy[:], 0.0)
         nc.vector.memset(w_planes[1][:].bitcast(I32), 0)
         nc.scalar.activation(out=warm_out[:], in_=warm_in[:], func=SIGMOID)
         make_identity(nc, identity[:])
@@ -106,10 +107,10 @@ def tile_lstmnetwork_pb_e_kernel(tc, h_layer0, w_ih_words, w_ih_scales, b_ih, b_
                 nc.sync.dma_start(out=x_rows[c][:, :, some], in_=rows[:, :, some])
 
         def load_planes(l):
-            groups = w_ih_scales[4 * l : 8]
+            groups = w_ih_scales[4 * l : 4 * l + 4]
             for quadrant in range(4):
                 nc.sync.dma_start(
-                    out=w_planes[l][32 * quadrant : 32 * quadrant + 32 - 16 * l, :].bitcast(I32),
+                    out=w_planes[l][32 * quadrant : 32 * quadrant + 16, :].bitcast(I32),
                     in_=groups[:, 4 * quadrant : 4 * quadrant + 4, :].bitcast(I32),
                 )
 
@@ -259,16 +260,16 @@ def tile_lstmnetwork_pb_e_kernel(tc, h_layer0, w_ih_words, w_ih_scales, b_ih, b_
                     rows = slice(tile * (P // PACK), (tile + 1) * (P // PACK))
                     nc.sync.dma_start(out=fetched[d][c][rows, :, :], in_=h_of[unit][:, k * NARROW : (k + 1) * NARROW])
 
-        def turn(unit, tiles_now):
+        def turn(unit, tiles_now, pool=turn_banks, tag="turned"):
             layer, d, first_tile, tiles, first_token, tokens = UNIT_LIST[unit]
-            h_rows = turn_banks.tile([P, tokens // P, len(tiles_now), P], F32, name="h_rows", tag="turned")
+            h_rows = pool.tile([P, tokens // P, len(tiles_now), P], F32, name="h_rows", tag=tag)
             for k, j in enumerate(tiles_now):
                 for i in range(tokens // P):
                     first = j * tokens + i * P
                     nc.tensor.transpose(h_rows[:, i, k, :], h_of[unit][:, first : first + P], identity[:])
             turned_of[unit] = h_rows
 
-        def store_rows(unit, tiles_now):
+        def store_rows(unit, tiles_now, copy=nc.vector.tensor_copy):
             layer, d, first_tile, tiles, first_token, tokens = UNIT_LIST[unit]
             width = PAIR * P if tiles == 1 or len(tiles_now) == PAIR else P
             k = first_tile % PAIR if tiles == 1 else 0
@@ -276,9 +277,7 @@ def tile_lstmnetwork_pb_e_kernel(tc, h_layer0, w_ih_words, w_ih_scales, b_ih, b_
                 result_of[d] = leave.tile([P, tokens // P, width], F32, name="result", tag="result")
             result = result_of[d]
             taken = len(tiles_now) * P
-            nc.vector.tensor_copy(
-                out=result[:, :, k * P : k * P + taken], in_=turned_of[unit][:].rearrange("p i j f -> p i (j f)")
-            )
+            copy(out=result[:, :, k * P : k * P + taken], in_=turned_of[unit][:].rearrange("p i j f -> p i (j f)"))
             if k * P + taken == width:
                 first = d * HIDDEN + (first_tile - k + tiles_now[0]) * P
                 nc.sync.dma_start(
@@ -289,16 +288,15 @@ def tile_lstmnetwork_pb_e_kernel(tc, h_layer0, w_ih_words, w_ih_scales, b_ih, b_
         early_work = {
             0: [(turn_input, (1, 0)), (turn_input, (1, 1))],
             2: [(quantise, (0, 0, 1)), (quantise, (0, 1, 1))],
-            7: [(group_hidden, (0, 1))],
-            10: [(group_hidden, (1, 0))],
+            7: [(quantise, (1, 1, 0))],
+            10: [(quantise, (1, 0, 1))],
         }
-        middle_work = {7: [(quantise, (1, 1, 0))], 10: [(quantise, (1, 0, 1))]}
         late_work = {
             1: [(group_input, (1, 0)), (group_input, (1, 1))],
-            5: [(group_hidden, (0, 0))],
-            6: [(quantise, (1, 0, 0))],
-            8: [(group_hidden, (1, 1))],
-            9: [(quantise, (1, 1, 1))],
+            5: [(group_hidden, (0, 0)), (quantise, (1, 0, 0))],
+            6: [(group_hidden, (0, 1))],
+            8: [(group_hidden, (1, 1)), (quantise, (1, 1, 1))],
+            9: [(group_hidden, (1, 0))],
         }
         first_step_for = {3: 2, 8: 7, 9: 7, 11: 10, 12: 10}
         at_once = (4, 7)
@@ -349,8 +347,6 @@ def tile_lstmnetwork_pb_e_kernel(tc, h_layer0, w_ih_words, w_ih_scales, b_ih, b_
             for j in range(tiles):
                 gate(step, 1, j)
                 cell_state(step, j)
-                if j == 0:
-                    run_work(middle_work, step)
             if waiting is not None:
                 squash(waiting, ALL)
             storing = list(to_store)
@@ -368,14 +364,12 @@ def tile_lstmnetwork_pb_e_kernel(tc, h_layer0, w_ih_words, w_ih_scales, b_ih, b_
                 if final:
                     squash(step, PIECES[j])
                     hidden(step, PIECES[j])
-                    for unit in to_store:
-                        store_rows(unit, range(PAIR))
-                    to_store.clear()
-                    if j == 1:
-                        store_rows(step, [0])
-                    turn(step, [j])
             if final:
-                store_rows(step, [1])
+                for unit in to_store:
+                    store_rows(unit, range(PAIR), nc.scalar.copy)
+                for j in range(tiles):
+                    turn(step, [j], gate_banks, "bank%d" % j)
+                    store_rows(step, [j], nc.vector.tensor_copy if j else nc.scalar.copy)
             elif step in at_once:
                 squash(step, ALL)
                 finish(step, PIECES)

@@ -92,9 +92,9 @@ def tile_lstmnetwork_pb_e_kernel(tc, h_layer0, w_ih_words, w_ih_scales, b_ih, b_
         warm_in = keep.tile([P, 1], F32)
         warm_out = keep.tile([P, 1], F32)
 
+        nc.vector.memset(dummy[:], 0.0)
         nc.vector.memset(warm_in[:], 0.0)
         nc.vector.memset(w_planes[0][:].bitcast(I32), 0)
-        nc.vector.memset(dummy[:], 0.0)
         nc.vector.memset(w_planes[1][:].bitcast(I32), 0)
         nc.scalar.activation(out=warm_out[:], in_=warm_in[:], func=SIGMOID)
         make_identity(nc, identity[:])
@@ -145,24 +145,32 @@ def tile_lstmnetwork_pb_e_kernel(tc, h_layer0, w_ih_words, w_ih_scales, b_ih, b_
         turned_input = {}
 
         def turn_input(c, k_pass):
-            turned = turn_banks.tile([P, 2, NARROW], F32, tag="turned")
+            turned = []
             for i in range(TOKEN_TILES):
+                if c == 0 and k_pass == 1:
+                    turned.append(gate_banks.tile([P, 2, P], F32, name="turned", tag="bank%d" % i))
+                elif c == 0:
+                    turned.append(turn_banks.tile([P, 2, P], F32, name="turned", tag="turned"))
+                elif i == 0:
+                    both = turn_banks.tile([P, 2, NARROW], F32, name="turned", tag="turned")
+                    turned = [both[:, :, j * P : (j + 1) * P] for j in range(TOKEN_TILES)]
                 pairs = x_rows[c][:, i, :].bitcast(F32)
                 for u in range(2):
                     nc.tensor.transpose(
-                        turned[:, u, i * P : (i + 1) * P],
+                        turned[i][:, u, :],
                         pairs[:, k_pass * (K_PASS // 2) + u : (k_pass + 1) * (K_PASS // 2) : 2],
                         identity[:],
                     )
-            turned_input[k_pass, c] = turned
+            turned_input[k_pass, c] = turned if c == 0 else [both]
 
         def group_input(c, k_pass):
             turned = turned_input[k_pass, c]
             grouped = stage.tile([P, NARROW, PACK], BF16, tag="grouped", align_bytes=64)
             if c == 0:
-                nc.scalar.copy(out=grouped[:].bitcast(F32), in_=turned[:].rearrange("p u n -> p n u"))
+                for i, copy in enumerate((nc.scalar.copy, nc.vector.tensor_copy)):
+                    copy(out=grouped[:, i * P : (i + 1) * P, :].bitcast(F32), in_=turned[i][:].rearrange("p u n -> p n u"))
             else:
-                nc.vector.tensor_copy(out=grouped[:].bitcast(F32), in_=turned[:].rearrange("p u n -> p n u"))
+                nc.vector.tensor_copy(out=grouped[:].bitcast(F32), in_=turned[0][:].rearrange("p u n -> p n u"))
             grouped_of[0, k_pass, c] = grouped
 
         def group_hidden(c, d):
@@ -308,11 +316,10 @@ def tile_lstmnetwork_pb_e_kernel(tc, h_layer0, w_ih_words, w_ih_scales, b_ih, b_
         keep_warm(5, gate_banks, "bank2")
         turn_input(0, 0)
         group_input(0, 0)
-        keep_warm(1, gate_banks, "bank2")
+        quantise(0, 0, 0)
         turn_input(0, 1)
         group_input(0, 1)
-        for k_pass in range(PASSES):
-            quantise(0, k_pass, 0)
+        quantise(0, 1, 0)
         keep_warm(3, gate_banks, "bank2")
         spread_biases()
         multiply(0)

@@ -100,6 +100,11 @@ def tile_lstmnetwork_pb_e_kernel(tc, h_layer0, w_ih_words, w_ih_scales, b_ih, b_
         make_identity(nc, identity[:])
         make_identity(nc, identity_bf16[:])
 
+        def load_token_tiles(c):
+            rows = h_layer0[c * NARROW : (c + 1) * NARROW, :].rearrange("(i p) f -> p i f", p=P)
+            for i in range(TOKEN_TILES):
+                nc.sync.dma_start(out=x_rows[c][:, i, :], in_=rows[:, i, :])
+
         def load_tokens(c):
             rows = h_layer0[c * NARROW : (c + 1) * NARROW, :].rearrange("(i p) f -> p i f", p=P)
             for k_pass in range(PASSES):
@@ -128,13 +133,13 @@ def tile_lstmnetwork_pb_e_kernel(tc, h_layer0, w_ih_words, w_ih_scales, b_ih, b_
             load_words(DIRECTIONS + d, BLOCK_G * HIDDEN, 2 * HIDDEN)
 
         load_tokens(0)
-        load_first_layer_words(0, 0, (BLOCK_I,))
+        load_words(0, BLOCK_I * HIDDEN, HIDDEN)
         load_planes(0)
         nc.sync.dma_start(out=bias_rows[0 : P // 2, :], in_=b_ih.rearrange("l d (r c) -> (l d r) c", c=P))
         nc.sync.dma_start(out=bias_rows[P // 2 : P, :], in_=b_hh.rearrange("l d (r c) -> (l d r) c", c=P))
-        load_first_layer_words(0, 0, (BLOCK_G, BLOCK_O))
-        load_first_layer_words(0, 1, (BLOCK_I, BLOCK_G, BLOCK_O))
-        load_tokens(1)
+        load_words(0, BLOCK_G * HIDDEN, HIDDEN)
+        load_words(0, BLOCK_O * HIDDEN, HIDDEN)
+        load_token_tiles(1)
         for pair in range(PAIRS):
             load_first_layer_words(1, pair, (BLOCK_I, BLOCK_G, BLOCK_O))
         load_planes(1)
@@ -206,11 +211,12 @@ def tile_lstmnetwork_pb_e_kernel(tc, h_layer0, w_ih_words, w_ih_scales, b_ih, b_
         def is_wide(unit):
             return 0 <= unit < UNITS and UNIT_LIST[unit][3] == 1
 
-        def multiply(unit):
+        def multiply(unit, gates=range(3)):
             layer, d, first_tile, tiles, first_token, tokens = UNIT_LIST[unit]
-            banks = [gate_banks.tile([P, tiles, tokens], F32, name="bank%d" % b, tag="bank%d" % b) for b in range(3)]
-            order = [(0, j) for j in range(tiles)] + [(1, j) for j in range(tiles)] + [(2, j) for j in range(tiles)]
-            for b, j in order:
+            banks = banks_of.setdefault(unit, [])
+            for b in gates:
+                banks.append(gate_banks.tile([P, tiles, tokens], F32, name="bank%d" % b, tag="bank%d" % b))
+            for b, j in [(b, j) for b in gates for j in range(tiles)]:
                 first = (BLOCK_I, BLOCK_G, BLOCK_O)[b] * HIDDEN + (first_tile + j) * P
                 for k_pass in range(PASSES):
                     in_layer = d * PASSES + k_pass
@@ -224,7 +230,6 @@ def tile_lstmnetwork_pb_e_kernel(tc, h_layer0, w_ih_words, w_ih_scales, b_ih, b_
                         start=(k_pass == 0),
                         stop=(k_pass == PASSES - 1),
                     )
-            banks_of[unit] = banks
 
         def gate(unit, b, j):
             layer, d, first_tile, tiles, first_token, tokens = UNIT_LIST[unit]
@@ -294,13 +299,10 @@ def tile_lstmnetwork_pb_e_kernel(tc, h_layer0, w_ih_words, w_ih_scales, b_ih, b_
                 )
 
         early_work = {
-            0: [(turn_input, (1, 0)), (turn_input, (1, 1))],
-            2: [(quantise, (0, 0, 1)), (quantise, (0, 1, 1))],
             7: [(quantise, (1, 1, 0))],
             10: [(quantise, (1, 0, 1))],
         }
         late_work = {
-            1: [(group_input, (1, 0)), (group_input, (1, 1))],
             5: [(group_hidden, (0, 0)), (quantise, (1, 0, 0))],
             6: [(group_hidden, (0, 1))],
             8: [(group_hidden, (1, 1)), (quantise, (1, 1, 1))],
@@ -322,8 +324,9 @@ def tile_lstmnetwork_pb_e_kernel(tc, h_layer0, w_ih_words, w_ih_scales, b_ih, b_
         quantise(0, 1, 0)
         keep_warm(3, gate_banks, "bank2")
         spread_biases()
-        multiply(0)
-        multiply(1)
+        for b in range(3):
+            multiply(0, [b])
+            multiply(1, [b])
         next_unit = 2
         to_turn, to_store = [], []
 
@@ -341,12 +344,32 @@ def tile_lstmnetwork_pb_e_kernel(tc, h_layer0, w_ih_words, w_ih_scales, b_ih, b_
                 to_store.append(unit)
             to_turn.clear()
 
+        turn_input(1, 0)
+        turn_input(1, 1)
+        for unit in range(2):
+            start_unit(unit)
+        for b in range(3):
+            for unit in range(2):
+                for j in range(PAIR):
+                    gate(unit, b, j)
+                    if b == 1:
+                        cell_state(unit, j)
+        for unit in range(2):
+            squash(unit, ALL)
+        group_input(1, 0)
+        group_input(1, 1)
+        quantise(0, 0, 1)
+        quantise(0, 1, 1)
+        for unit in range(2):
+            finish(unit, [ALL])
+        multiply(2)
+        next_unit = 3
         waiting = None
-        for step in range(UNITS):
+        for step in range(2, UNITS):
             tiles = UNIT_LIST[step][3]
             final = step == UNITS - 1
             start_unit(step)
-            if step == 6:
+            if step == 5:
                 load_second_layer_words(1)
             run_work(early_work, step)
             for j in range(tiles):

from contextlib import ExitStack

import concourse.mybir as mybir
from concourse.masks import make_identity

F32 = mybir.dt.float32
BF16 = mybir.dt.bfloat16
I32 = mybir.dt.int32
U32 = mybir.dt.uint32
U8 = mybir.dt.uint8
FP8X4 = mybir.dt.float8_e4m3fn_x4
SIGMOID = mybir.ActivationFunctionType.Sigmoid
TANH = mybir.ActivationFunctionType.Tanh
MULT = mybir.AluOpType.mult
ADD = mybir.AluOpType.add

P = 128
PACK = 4
K_PASS = P * PACK
TOKENS = 512
FEATURES = 1024
HIDDEN = 512
LAYERS = 2
DIRECTIONS = 2
PASSES = FEATURES // K_PASS
GROUPS_PER_LAYER = DIRECTIONS * PASSES
GATE_BLOCKS = 4
BLOCK_I, BLOCK_G, BLOCK_O = 0, 2, 3
TILES_PER_BLOCK = HIDDEN // P
NARROW = 256
CHUNKS = TOKENS // NARROW
TOKEN_TILES = NARROW // P
PAIR = 2
PAIRS = TILES_PER_BLOCK // PAIR
COLUMNS = 512
AHEAD = 2

FLOPS = 2 * TOKENS * FEATURES * 3 * HIDDEN * LAYERS * DIRECTIONS
BYTES = (
    TOKENS * FEATURES * 2
    + LAYERS * DIRECTIONS * FEATURES * 3 * HIDDEN
    + LAYERS * DIRECTIONS * (FEATURES // 32) * 3 * HIDDEN
    + 2 * LAYERS * DIRECTIONS * 3 * HIDDEN * 2
    + TOKENS * FEATURES * 4
)


def list_units():
    units = []
    for layer in range(LAYERS):
        for token in (0, NARROW):
            if token:
                units += [(layer, 1, tile, 1, 0, TOKENS) for tile in range(PAIR, TILES_PER_BLOCK)]
            units += [(layer, d, pair * PAIR, PAIR, token, NARROW) for d, pair in (((1, 0), (0, 0), (0, 1)) if token else ((0, 0), (0, 1), (1, 0)))]
    return units


UNIT_LIST = list_units()
UNITS = len(UNIT_LIST)
UNITS_PER_LAYER = UNITS // LAYERS


def tile_lstmnetwork_pb_e_kernel(tc, h_layer0, w_ih_words, w_ih_scales, b_ih, b_hh, out):
    nc = tc.nc
    out_rows = out.rearrange("b c f -> (b c) f")
    with ExitStack() as ctx:
        ctx.enter_context(tc.manual_schedule())
        keep = ctx.enter_context(tc.tile_pool(name="keep", bufs=1))
        stage = ctx.enter_context(tc.tile_pool(name="stage", bufs=2))
        work = ctx.enter_context(tc.tile_pool(name="work", bufs=3))
        leave = ctx.enter_context(tc.tile_pool(name="leave", bufs=5))
        gate_banks = ctx.enter_context(tc.psum_pool(name="gate_banks", bufs=AHEAD))
        turn_banks = ctx.enter_context(tc.psum_pool(name="turn_banks", bufs=2))

        x_rows = [keep.tile([P, TOKEN_TILES, FEATURES], BF16, name="x_rows%d" % c) for c in range(CHUNKS)]
        w_words = [
            keep.tile([P, PASSES, GATE_BLOCKS * HIDDEN * PACK], U8, name="w_words%d" % e, align_bytes=64)
            for e in range(LAYERS * DIRECTIONS)
        ]
        w_planes = [keep.tile([P, GATE_BLOCKS * HIDDEN], U8, name="w_planes%d" % l, align_bytes=64) for l in range(LAYERS)]
        h_words = keep.tile([P, LAYERS * PASSES, TOKENS], U32, align_bytes=64)
        h_planes = keep.tile([P, LAYERS * PASSES, TOKENS], U8, align_bytes=64)
        fetched = [
            [keep.tile([P, PACK, NARROW], BF16, name="fetched%d%d" % (d, c)) for c in range(CHUNKS)] for d in range(DIRECTIONS)
        ]
        identity = keep.tile([P, P], F32)
        bias_rows = keep.tile([P, P], BF16)
        identity_bf16 = keep.tile([P, P], BF16)
        bias_ih = keep.tile([P, P // 2], F32)
        bias = keep.tile([P, P // 2], F32)
        dummy = keep.tile([P, HIDDEN], BF16)
        warm_in = keep.tile([P, 1], F32)
        warm_out = keep.tile([P, 1], F32)

        nc.vector.memset(dummy[:], 0.0)
        nc.vector.memset(warm_in[:], 0.0)
        nc.vector.memset(w_planes[0][:].bitcast(I32), 0)
        nc.vector.memset(w_planes[1][:].bitcast(I32), 0)
        nc.scalar.activation(out=warm_out[:], in_=warm_in[:], func=SIGMOID)
        make_identity(nc, identity[:])
        make_identity(nc, identity_bf16[:])

        def load_token_tiles(c):
            rows = h_layer0[c * NARROW : (c + 1) * NARROW, :].rearrange("(i p) f -> p i f", p=P)
            for i in range(TOKEN_TILES):
                nc.sync.dma_start(out=x_rows[c][:, i, :], in_=rows[:, i, :])

        def load_tokens(c):
            rows = h_layer0[c * NARROW : (c + 1) * NARROW, :].rearrange("(i p) f -> p i f", p=P)
            for k_pass in range(PASSES):
                some = slice(k_pass * K_PASS, (k_pass + 1) * K_PASS)
                nc.sync.dma_start(out=x_rows[c][:, :, some], in_=rows[:, :, some])

        def load_planes(l):
            groups = w_ih_scales[4 * l : 4 * l + 4]
            for quadrant in range(4):
                nc.sync.dma_start(
                    out=w_planes[l][32 * quadrant : 32 * quadrant + 16, :].bitcast(I32),
                    in_=groups[:, 4 * quadrant : 4 * quadrant + 4, :].bitcast(I32),
                )

        def load_words(e, first, columns):
            some = slice(first * PACK, (first + columns) * PACK)
            in_hbm = w_ih_words[e * PASSES : (e + 1) * PASSES].rearrange("g p n t -> p g (n t)")
            nc.sync.dma_start(out=w_words[e][:, :, some].bitcast(I32), in_=in_hbm[:, :, some].bitcast(I32))

        def load_first_layer_words(d, pair, blocks):
            for block in blocks:
                load_words(d, block * HIDDEN + pair * PAIR * P, PAIR * P)

        def load_second_layer_words(d):
            load_words(DIRECTIONS + d, BLOCK_I * HIDDEN, HIDDEN)
            load_words(DIRECTIONS + d, BLOCK_G * HIDDEN, 2 * HIDDEN)

        load_tokens(0)
        load_words(0, BLOCK_I * HIDDEN, HIDDEN)
        load_planes(0)
        nc.sync.dma_start(out=bias_rows[0 : P // 2, :], in_=b_ih.rearrange("l d (r c) -> (l d r) c", c=P))
        nc.sync.dma_start(out=bias_rows[P // 2 : P, :], in_=b_hh.rearrange("l d (r c) -> (l d r) c", c=P))
        load_words(0, BLOCK_G * HIDDEN, HIDDEN)
        load_words(0, BLOCK_O * HIDDEN, HIDDEN)
        load_token_tiles(1)
        for pair in range(PAIRS):
            load_first_layer_words(1, pair, (BLOCK_I, BLOCK_G, BLOCK_O))
        load_planes(1)
        load_second_layer_words(0)

        grouped_of = {}

        turned_input = {}

        def turn_input(c, k_pass):
            turned = []
            for i in range(TOKEN_TILES):
                if c == 0 and k_pass == 1:
                    turned.append(gate_banks.tile([P, 2, P], F32, name="turned", tag="bank%d" % i))
                elif c == 0:
                    turned.append(turn_banks.tile([P, 2, P], F32, name="turned", tag="turned"))
                elif i == 0:
                    both = turn_banks.tile([P, 2, NARROW], F32, name="turned", tag="turned")
                    turned = [both[:, :, j * P : (j + 1) * P] for j in range(TOKEN_TILES)]
                pairs = x_rows[c][:, i, :].bitcast(F32)
                for u in range(2):
                    nc.tensor.transpose(
                        turned[i][:, u, :],
                        pairs[:, k_pass * (K_PASS // 2) + u : (k_pass + 1) * (K_PASS // 2) : 2],
                        identity[:],
                    )
            turned_input[k_pass, c] = turned if c == 0 else [both]

        def group_input(c, k_pass):
            turned = turned_input[k_pass, c]
            grouped = stage.tile([P, NARROW, PACK], BF16, tag="grouped", align_bytes=64)
            if c == 0:
                for i, copy in enumerate((nc.scalar.copy, nc.vector.tensor_copy)):
                    copy(out=grouped[:, i * P : (i + 1) * P, :].bitcast(F32), in_=turned[i][:].rearrange("p u n -> p n u"))
            else:
                nc.vector.tensor_copy(out=grouped[:].bitcast(F32), in_=turned[0][:].rearrange("p u n -> p n u"))
            grouped_of[0, k_pass, c] = grouped

        def group_hidden(c, d):
            grouped = stage.tile([P, NARROW, PACK], BF16, tag="grouped", align_bytes=64)
            nc.vector.tensor_copy(out=grouped[:], in_=fetched[d][c][:].rearrange("p t n -> p n t"))
            grouped_of[1, d, c] = grouped

        def quantise(layer, k_pass, c):
            some = slice(c * NARROW, (c + 1) * NARROW)
            nc.vector.quantize_mx(
                out=h_words[:, layer * PASSES + k_pass, some].bitcast(FP8X4),
                scales=h_planes[:, layer * PASSES + k_pass, some],
                in_=grouped_of[layer, k_pass, c][:].rearrange("p n t -> p (n t)"),
            )

        def spread_biases():
            bias_turned = turn_banks.tile([P, P], BF16, tag="turned")
            nc.tensor.transpose(bias_turned[:], bias_rows[:], identity_bf16[:])
            nc.vector.tensor_copy(out=bias_ih[:], in_=bias_turned[:, 0 : P // 2])
            nc.vector.tensor_tensor(out=bias[:], in0=bias_ih[:], in1=bias_turned[:, P // 2 : P], op=ADD)

        def keep_warm(count, pool, tag):
            unread = pool.tile([P, HIDDEN], F32, name="unread", tag=tag)
            for n in range(count):
                nc.tensor.matmul(unread[:], lhsT=dummy[:, 0:P], rhs=dummy[:], start=True, stop=True)

        banks_of = {}
        acts_of = {}
        h_of = {}
        turned_of = {}
        result_of = {}

        def is_wide(unit):
            return 0 <= unit < UNITS and UNIT_LIST[unit][3] == 1

        def multiply(unit, gates=range(3)):
            layer, d, first_tile, tiles, first_token, tokens = UNIT_LIST[unit]
            banks = banks_of.setdefault(unit, [])
            for b in gates:
                banks.append(gate_banks.tile([P, tiles, tokens], F32, name="bank%d" % b, tag="bank%d" % b))
            for b, j in [(b, j) for b in gates for j in range(tiles)]:
                first = (BLOCK_I, BLOCK_G, BLOCK_O)[b] * HIDDEN + (first_tile + j) * P
                for k_pass in range(PASSES):
                    in_layer = d * PASSES + k_pass
                    some = slice(first_token, first_token + tokens)
                    nc.tensor.matmul_mx(
                        out=banks[b][:, j, :],
                        lhsT=w_words[layer * DIRECTIONS + d][:, k_pass, first * PACK : (first + P) * PACK].bitcast(FP8X4),
                        lhsT_scale=w_planes[layer][4 * in_layer : P, first : first + P],
                        rhs=h_words[:, layer * PASSES + k_pass, some].bitcast(FP8X4),
                        rhs_scale=h_planes[:, layer * PASSES + k_pass, some],
                        start=(k_pass == 0),
                        stop=(k_pass == PASSES - 1),
                    )

        def gate(unit, b, j):
            layer, d, first_tile, tiles, first_token, tokens = UNIT_LIST[unit]
            r = ((layer * DIRECTIONS + d) * GATE_BLOCKS + (BLOCK_I, BLOCK_G, BLOCK_O)[b]) * TILES_PER_BLOCK + first_tile + j
            nc.scalar.activation(
                out=acts_of[unit][b][:, j * tokens : (j + 1) * tokens],
                in_=banks_of[unit][b][:, j, :],
                func=(SIGMOID, TANH, SIGMOID)[b],
                bias=bias[:, r : r + 1],
            )

        def start_unit(unit):
            acts_of[unit] = [work.tile([P, COLUMNS], F32, name="work%d" % k, tag="work%d" % k) for k in range(5)]
            if unit < UNITS_PER_LAYER:
                h_of[unit] = keep.tile([P, COLUMNS], BF16, name="h_first%d" % unit)
            else:
                h_of[unit] = leave.tile([P, COLUMNS], F32, name="h_last", tag="h_last")

        def cell_state(unit, j):
            i_act, g_act, o_act, cell, cell_tanh = acts_of[unit]
            tokens = UNIT_LIST[unit][5]
            some = slice(j * tokens, (j + 1) * tokens)
            nc.vector.tensor_tensor(out=cell[:, some], in0=i_act[:, some], in1=g_act[:, some], op=MULT)

        def squash(unit, some):
            i_act, g_act, o_act, cell, cell_tanh = acts_of[unit]
            nc.scalar.activation(out=cell_tanh[:, some], in_=cell[:, some], func=TANH)

        def hidden(unit, some):
            i_act, g_act, o_act, cell, cell_tanh = acts_of[unit]
            nc.vector.tensor_tensor(out=h_of[unit][:, some], in0=o_act[:, some], in1=cell_tanh[:, some], op=MULT)

        ALL = slice(0, COLUMNS)
        PIECES = [slice(0, NARROW), slice(NARROW, COLUMNS)]

        def hand_over(unit, piece):
            layer, d, first_tile, tiles, first_token, tokens = UNIT_LIST[unit]
            for k in range(COLUMNS // NARROW):
                if piece.start <= k * NARROW < piece.stop:
                    tile, c = (first_tile, k) if tiles == 1 else (first_tile + k, first_token // NARROW)
                    rows = slice(tile * (P // PACK), (tile + 1) * (P // PACK))
                    nc.sync.dma_start(out=fetched[d][c][rows, :, :], in_=h_of[unit][:, k * NARROW : (k + 1) * NARROW])

        def turn(unit, tiles_now, pool=turn_banks, tag="turned"):
            layer, d, first_tile, tiles, first_token, tokens = UNIT_LIST[unit]
            h_rows = pool.tile([P, tokens // P, len(tiles_now), P], F32, name="h_rows", tag=tag)
            for k, j in enumerate(tiles_now):
                for i in range(tokens // P):
                    first = j * tokens + i * P
                    nc.tensor.transpose(h_rows[:, i, k, :], h_of[unit][:, first : first + P], identity[:])
            turned_of[unit] = h_rows

        def store_rows(unit, tiles_now, copy=nc.vector.tensor_copy):
            layer, d, first_tile, tiles, first_token, tokens = UNIT_LIST[unit]
            width = PAIR * P if tiles == 1 or len(tiles_now) == PAIR else P
            k = first_tile % PAIR if tiles == 1 else 0
            if k == 0:
                result_of[d] = leave.tile([P, tokens // P, width], F32, name="result", tag="result")
            result = result_of[d]
            taken = len(tiles_now) * P
            copy(out=result[:, :, k * P : k * P + taken], in_=turned_of[unit][:].rearrange("p i j f -> p i (j f)"))
            if k * P + taken == width:
                first = d * HIDDEN + (first_tile - k + tiles_now[0]) * P
                nc.sync.dma_start(
                    out=out_rows[first_token : first_token + tokens, first : first + width].rearrange("(i p) f -> p i f", p=P),
                    in_=result[:],
                )

        early_work = {
            7: [(quantise, (1, 1, 0))],
            10: [(quantise, (1, 0, 1))],
        }
        late_work = {
            5: [(group_hidden, (0, 0)), (quantise, (1, 0, 0))],
            6: [(group_hidden, (0, 1))],
            8: [(group_hidden, (1, 1)), (quantise, (1, 1, 1))],
            9: [(group_hidden, (1, 0))],
        }
        first_step_for = {3: 2, 8: 7, 9: 7, 11: 10, 12: 10}
        at_once = (4, 7)

        def run_work(table, step):
            for work_item, arguments in table.get(step, []):
                work_item(*arguments)

        keep_warm(5, gate_banks, "bank2")
        turn_input(0, 0)
        group_input(0, 0)
        quantise(0, 0, 0)
        turn_input(0, 1)
        group_input(0, 1)
        quantise(0, 1, 0)
        keep_warm(3, gate_banks, "bank2")
        spread_biases()
        for b in range(3):
            multiply(0, [b])
            multiply(1, [b])
        next_unit = 2
        to_turn, to_store = [], []

        def finish(unit, pieces):
            for piece in pieces:
                hidden(unit, piece)
                if unit < UNITS_PER_LAYER:
                    hand_over(unit, piece)
            if unit >= UNITS_PER_LAYER:
                to_turn.append(unit)

        def turn_all():
            for unit in to_turn:
                turn(unit, range(UNIT_LIST[unit][3]))
                to_store.append(unit)
            to_turn.clear()

        turn_input(1, 0)
        turn_input(1, 1)
        for unit in range(2):
            start_unit(unit)
        for b in range(3):
            for unit in range(2):
                for j in range(PAIR):
                    gate(unit, b, j)
                    if b == 1:
                        cell_state(unit, j)
        for unit in range(2):
            squash(unit, ALL)
        group_input(1, 0)
        group_input(1, 1)
        quantise(0, 0, 1)
        quantise(0, 1, 1)
        for unit in range(2):
            finish(unit, [ALL])
        multiply(2)
        next_unit = 3
        waiting = None
        for step in range(2, UNITS):
            tiles = UNIT_LIST[step][3]
            final = step == UNITS - 1
            start_unit(step)
            if step == 5:
                load_second_layer_words(1)
            run_work(early_work, step)
            for j in range(tiles):
                gate(step, 0, j)
            for j in range(tiles):
                gate(step, 1, j)
                cell_state(step, j)
            if waiting is not None:
                squash(waiting, ALL)
            storing = list(to_store)
            to_store.clear()
            if waiting is not None:
                finish(waiting, [ALL])
                waiting = None
            if next_unit == UNITS:
                turn_all()
            for unit in storing:
                store_rows(unit, range(UNIT_LIST[unit][3]))
            run_work(late_work, step)
            for j in range(tiles):
                gate(step, 2, j)
                if final:
                    squash(step, PIECES[j])
                    hidden(step, PIECES[j])
            if final:
                for unit in to_store:
                    store_rows(unit, range(PAIR), nc.scalar.copy)
                for j in range(tiles):
                    turn(step, [j], gate_banks, "bank%d" % j)
                    store_rows(step, [j], nc.vector.tensor_copy if j else nc.scalar.copy)
            elif step in at_once:
                squash(step, ALL)
                finish(step, PIECES)
            else:
                waiting = step
            while next_unit < UNITS and first_step_for.get(next_unit, next_unit - AHEAD) <= step:
                multiply(next_unit)
                next_unit += 1
                if next_unit == UNITS_PER_LAYER:
                    keep_warm(8, turn_banks, "turned")
            turn_all()
            if step == 8:
                keep_warm(5, turn_banks, "turned")
